import numpy as np
import ml_dtypes


def mxq(x, axis, fmt="e4m3"):
    dtype, down = {"e4m3": (ml_dtypes.float8_e4m3fn, 7), "e5m2": (ml_dtypes.float8_e5m2, 14)}[fmt]
    v = np.moveaxis(np.asarray(x, np.float32).astype(ml_dtypes.bfloat16).astype(np.float64), axis, -1)
    blocks = v.reshape(v.shape[:-1] + (-1, 32))
    amax = np.abs(blocks).max(-1, keepdims=True)
    byte = np.maximum(np.where(amax > 0, np.frexp(amax)[1] - 1 + 127, 0) - down, 1)
    scale = np.exp2(byte - 127.0)
    codes = (blocks / scale).astype(np.float32).astype(dtype).astype(np.float64)
    return np.moveaxis((codes * scale).reshape(v.shape), -1, axis)


WIDE = False


def mx_kscale(k):
    if not WIDE:
        return np.ones(k)
    levels = np.array([10, -10, 5, -5, 0])
    a = np.random.permutation(np.resize(levels, k // 512 * 4)).reshape(k // 512, 4)
    idx = np.arange(k)
    return np.exp2(a[idx // 512, idx % 128 // 32])


BF16 = ml_dtypes.bfloat16


def bf(x):
    return np.asarray(x, np.float32).astype(BF16)


def f64(x):
    return np.asarray(x).astype(np.float64)


B, N, D_IN, H, D_HEAD, D_EXPAND = 4, 1024, 512, 1, 128, 512
D_V = D_IN * H
EPS = 1e-5


def feature_norm(x, gamma, beta):
    mean = x.mean(axis=1, keepdims=True)
    var = x.var(axis=1, keepdims=True)
    return gamma * (x - mean) / np.sqrt(var + EPS) + beta


def setup_inputs():
    t = mx_kscale(D_V)
    s = mx_kscale(D_IN)
    return {"attn_out": bf(5.0 * np.random.standard_normal((B, N, D_V)) * t),
            "x": bf(1.5 * np.random.standard_normal((B, N, D_IN))),
            "W_merge": bf(np.random.standard_normal((D_V, D_IN)) * 0.2 / np.sqrt(D_V) / t[:, None]),
            "b_merge": bf(0.3 * np.random.standard_normal(D_IN)),
            "gamma2": bf((1.0 + 0.1 * np.random.standard_normal((1, 1, D_IN))) * s),
            "beta2": bf(0.2 * np.random.standard_normal((1, 1, D_IN)) * s),
            "W1": bf(np.random.standard_normal((D_IN, D_EXPAND)) / np.sqrt(D_IN) / s[:, None]),
            "b1": bf(0.2 * np.random.standard_normal(D_EXPAND))}


def reference(attn_out, x, W_merge, b_merge, gamma2, beta2, W1, b1):
    x2 = f64(x) + (mxq(f64(attn_out), 2, "e4m3") @ mxq(f64(W_merge), 0, "e4m3")) + f64(b_merge)
    xn = feature_norm(x2, f64(gamma2), f64(beta2))
    ffh = (mxq(xn, 2, "e4m3") @ mxq(f64(W1), 0, "e4m3")) + f64(b1)
    return x2, ffh

@@ -1,0 +1,333 @@
+import concourse.mybir as mybir
+from concourse.masks import make_identity
+
+F32 = mybir.dt.float32
+BF16 = mybir.dt.bfloat16
+U32 = mybir.dt.uint32
+U8 = mybir.dt.uint8
+FP8X4 = mybir.dt.float8_e4m3fn_x4
+ADD = mybir.AluOpType.add
+MULT = mybir.AluOpType.mult
+ACT = mybir.ActivationFunctionType
+
+P = 128
+PACK = 4
+BATCH = 4
+TOKENS = 1024
+FEATS = 512
+TILES = TOKENS // P
+HALF_TILES = TILES // 2
+HALF = HALF_TILES * P
+EPS = 1e-5
+
+FLOPS = 2 * 2 * BATCH * TOKENS * FEATS * FEATS
+
+
+def quantise_weight(nc, stage, keep, raw, label):
+    grouped = stage.tile([P, FEATS, PACK], BF16, align_bytes=64, name="grouped_" + label)
+    nc.vector.tensor_copy(out=grouped[:], in_=raw[:].rearrange("p t c -> p c t"))
+    codes = keep.tile([P, FEATS], U32, align_bytes=64, name="codes_" + label)
+    scales = keep.tile([P, FEATS], U8, align_bytes=64, name="scales_" + label)
+    nc.vector.quantize_mx(
+        out=codes[:].bitcast(FP8X4),
+        scales=scales[:],
+        in_=grouped[:].rearrange("p c t -> p (c t)"),
+    )
+    return codes, scales
+
+
+def tile_attentionblock_pc_t_kernel(
+    tc, attn_out, x, W_merge, b_merge, gamma2, beta2, W1, b1, out_0, out_1
+):
+    nc = tc.nc
+    with (
+        tc.tile_pool(name="keep", bufs=1) as keep,
+        tc.tile_pool(name="wstage", bufs=1) as wstage,
+        tc.tile_pool(name="inputs", bufs=3) as inputs,
+        tc.tile_pool(name="feat", bufs=2) as feat,
+        tc.tile_pool(name="mx", bufs=2) as mx,
+        tc.tile_pool(name="outs", bufs=3) as outs,
+        tc.tile_pool(name="small", bufs=2) as small,
+        tc.psum_pool(name="psum_tr", bufs=2) as psum_tr,
+        tc.psum_pool(name="psum_mm", bufs=4) as psum_mm,
+        tc.psum_pool(name="psum_x2", bufs=2) as psum_x2,
+        tc.manual_schedule(),
+    ):
+        attn_sb = {}
+        x_sb = {}
+        xT = {}
+        x2T = {}
+        sums = {}
+        neg_mean = {}
+        std = {}
+        gain = {}
+        shift = {}
+        xn = {}
+        a_grouped = {}
+        a_codes = {}
+        a_scales = {}
+        n_codes = {}
+        n_scales = {}
+        ff_ps = {}
+
+        def load_batch(b):
+            a_in = inputs.tile([P, TILES * FEATS], BF16, name="a_in")
+            x_in = inputs.tile([P, TILES * FEATS], BF16, name="x_in")
+            nc.sync.dma_start(out=a_in[:], in_=attn_out[b].rearrange("(p i) f -> p (i f)", i=TILES))
+            nc.sync.dma_start(out=x_in[:], in_=x[b].rearrange("(p i) f -> p (i f)", i=TILES))
+            attn_sb[b] = a_in
+            x_sb[b] = x_in
+
+        def transpose_attn(b):
+            a32 = attn_sb[b][:].bitcast(F32)
+            for h in range(2):
+                grouped = mx.tile([P, HALF * PACK], BF16, align_bytes=64, name="a_grouped")
+                a_grouped[b, h] = grouped
+                a_words = grouped[:].bitcast(F32).rearrange("p (r u) -> p r u", u=2)
+                for pair in range(HALF_TILES // 2):
+                    at_ps = psum_tr.tile([P, 2, 2 * P], F32, tag="tr")
+                    for j in range(2):
+                        i = h * HALF_TILES + pair * 2 + j
+                        for u in range(2):
+                            nc.tensor.transpose(
+                                out=at_ps[:, u, j * P : (j + 1) * P],
+                                in_=a32[:, i * 256 + u * P : i * 256 + (u + 1) * P],
+                                identity=ident_f32[:],
+                            )
+                    nc.scalar.copy(
+                        out=a_words[:, pair * 2 * P : (pair + 1) * 2 * P, :],
+                        in_=at_ps[:].rearrange("p u r -> p r u"),
+                    )
+
+        def transpose_x(b):
+            x_t = feat.tile([P, PACK, TOKENS], BF16, name="xT")
+            xT[b] = x_t
+            for t in range(PACK):
+                xt_ps = psum_tr.tile([P, TOKENS], BF16, tag="tr")
+                for i in range(TILES):
+                    nc.tensor.transpose(
+                        out=xt_ps[:, i * P : (i + 1) * P],
+                        in_=x_sb[b][:, i * FEATS + t * P : i * FEATS + (t + 1) * P],
+                        identity=ident_bf[:],
+                    )
+                nc.scalar.copy(out=x_t[:, t, :], in_=xt_ps[:])
+
+        def quantise_attn(b):
+            for h in range(2):
+                codes = mx.tile([P, HALF], U32, align_bytes=64, name="a_codes")
+                scales = mx.tile([P, HALF], U8, align_bytes=64, name="a_scales")
+                nc.vector.quantize_mx(
+                    out=codes[:].bitcast(FP8X4), scales=scales[:], in_=a_grouped[b, h][:]
+                )
+                a_codes[b, h] = codes
+                a_scales[b, h] = scales
+            x2_t = feat.tile([P, PACK, TOKENS], F32, name="x2T")
+            x2T[b] = x2_t
+            sums_b = small.tile([P, PACK, 2], F32, name="sums")
+            sums[b] = sums_b
+
+        def first_matmul(b, h):
+            cols = slice(h * HALF, (h + 1) * HALF)
+            for t in range(PACK):
+                y_ps = psum_mm.tile([P, HALF], F32, tag="mm")
+                nc.tensor.matmul_mx(
+                    out=y_ps[:],
+                    lhsT=wm_codes[:, t * P : (t + 1) * P].bitcast(FP8X4),
+                    lhsT_scale=wm_scales[:, t * P : (t + 1) * P],
+                    rhs=a_codes[b, h][:].bitcast(FP8X4),
+                    rhs_scale=a_scales[b, h][:],
+                    start=True,
+                    stop=True,
+                )
+                nc.vector.scalar_tensor_tensor(
+                    out=x2T[b][:, t, cols],
+                    in0=y_ps[:],
+                    scalar=bias_m[:, t : t + 1],
+                    in1=xT[b][:, t, cols],
+                    op0=ADD,
+                    op1=ADD,
+                    accum_out=sums[b][:, t, h : h + 1],
+                )
+
+        def stats_begin(b):
+            nm = small.tile([P, PACK], F32, name="neg_mean")
+            neg_mean[b] = nm
+            nc.vector.tensor_tensor(out=nm[:], in0=sums[b][:, :, 0], in1=sums[b][:, :, 1], op=ADD)
+            nc.vector.tensor_scalar_mul(out=nm[:], in0=nm[:], scalar1=-1.0 / TOKENS)
+            ssq = small.tile([P, PACK], F32, name="ssq")
+            for t in range(PACK):
+                squares = feat.tile([P, TOKENS], BF16, name="squares")
+                nc.scalar.activation(
+                    out=squares[:],
+                    in_=x2T[b][:, t, :],
+                    func=ACT.Square,
+                    bias=nm[:, t : t + 1],
+                    scale=1.0,
+                    accum_out=ssq[:, t : t + 1],
+                )
+            sd = small.tile([P, PACK], F32, name="std")
+            std[b] = sd
+            nc.scalar.activation(
+                out=sd[:], in_=ssq[:], func=ACT.Sqrt, bias=eps_col[:], scale=1.0 / TOKENS
+            )
+
+        def stats_end(b):
+            g = small.tile([P, PACK], F32, name="gain")
+            gain[b] = g
+            nc.vector.reciprocal(out=g[:], in_=std[b][:])
+            nc.vector.tensor_tensor(out=g[:], in0=g[:], in1=gamma, op=MULT)
+            sh = small.tile([P, PACK], F32, name="shift")
+            shift[b] = sh
+            nc.vector.tensor_tensor(out=sh[:], in0=neg_mean[b][:], in1=g[:], op=MULT)
+            nc.vector.tensor_tensor(out=sh[:], in0=sh[:], in1=beta, op=ADD)
+
+        def norm(b):
+            xn_b = feat.tile([P, PACK, TOKENS], BF16, name="xn")
+            xn[b] = xn_b
+            for h in range(2):
+                cols = slice(h * HALF, (h + 1) * HALF)
+                for t in range(PACK):
+                    nc.gpsimd.tensor_scalar(
+                        out=xn_b[:, t, cols],
+                        in0=x2T[b][:, t, cols],
+                        scalar1=gain[b][:, t : t + 1],
+                        scalar2=shift[b][:, t : t + 1],
+                        op0=MULT,
+                        op1=ADD,
+                    )
+
+        def x2_tiles(b, x2_out, h, tiles):
+            for j in tiles:
+                i = h * HALF_TILES + j
+                x2_ps = psum_x2.tile([P, FEATS], F32, tag="x2")
+                for t in range(PACK):
+                    nc.tensor.transpose(
+                        out=x2_ps[:, t * P : (t + 1) * P],
+                        in_=x2T[b][:, t, i * P : (i + 1) * P],
+                        identity=ident_f32[:],
+                    )
+                nc.scalar.copy(out=x2_out[:, j, :], in_=x2_ps[:])
+
+        def store_half(dram, b, h, tile_sb):
+            view = dram[b].rearrange("(p i) f -> p i f", i=TILES)
+            nc.sync.dma_start(out=view[:, h * HALF_TILES : (h + 1) * HALF_TILES, :], in_=tile_sb[:])
+
+        def second_matmul(b, h):
+            n_grouped = mx.tile([P, HALF, PACK], BF16, align_bytes=64, name="n_grouped")
+            nc.vector.tensor_copy(
+                out=n_grouped[:],
+                in_=xn[b][:, :, h * HALF : (h + 1) * HALF].rearrange("p t r -> p r t"),
+            )
+            codes = mx.tile([P, HALF], U32, align_bytes=64, name="n_codes")
+            scales = mx.tile([P, HALF], U8, align_bytes=64, name="n_scales")
+            nc.vector.quantize_mx(
+                out=codes[:].bitcast(FP8X4),
+                scales=scales[:],
+                in_=n_grouped[:].rearrange("p r t -> p (r t)"),
+            )
+            for j in range(HALF_TILES):
+                ps = psum_mm.tile([P, FEATS], F32, tag="mm", name="ff_ps")
+                ff_ps[b, h, j] = ps
+                nc.tensor.matmul_mx(
+                    out=ps[:],
+                    lhsT=codes[:, j * P : (j + 1) * P].bitcast(FP8X4),
+                    lhsT_scale=scales[:, j * P : (j + 1) * P],
+                    rhs=w1_codes[:].bitcast(FP8X4),
+                    rhs_scale=w1_scales[:],
+                    start=True,
+                    stop=True,
+                )
+
+        def second_out(b, h):
+            ff_out = outs.tile([P, HALF_TILES, FEATS], F32, name="ff_out")
+            for j in range(HALF_TILES):
+                nc.vector.tensor_tensor(
+                    out=ff_out[:, j, :], in0=ff_ps[b, h, j][:], in1=b1_all[:], op=ADD
+                )
+            store_half(out_1, b, h, ff_out)
+
+        wm_raw = wstage.tile([P, PACK, FEATS], BF16)
+        nc.sync.dma_start(
+            out=wm_raw[:].rearrange("q (u e) c -> q u (e c)", u=2),
+            in_=W_merge.rearrange("(u q e) c -> q u (e c)", u=2, e=2),
+        )
+        vec_rows = keep.tile([P, P], BF16)
+        b1_row = keep.tile([P, FEATS], BF16)
+        w1_raw = wstage.tile([P, PACK, FEATS], BF16)
+        nc.gpsimd.memset(vec_rows[:], 0.0)
+        nc.gpsimd.memset(b1_row[:], 0.0)
+        nc.sync.dma_start(out=vec_rows[0:4, :], in_=b_merge.rearrange("(t p) -> t p", p=P))
+        nc.sync.dma_start(out=vec_rows[4:8, :], in_=gamma2.rearrange("a b (t p) -> (a b t) p", p=P))
+        nc.sync.dma_start(out=vec_rows[8:12, :], in_=beta2.rearrange("a b (t p) -> (a b t) p", p=P))
+        load_batch(0)
+        nc.sync.dma_start(out=w1_raw[:], in_=W1.rearrange("(t p) c -> p t c", p=P))
+        nc.sync.dma_start(out=b1_row[0:1, :], in_=b1.rearrange("(o n) -> o n", o=1))
+        load_batch(1)
+        load_batch(2)
+
+        ident_f32 = keep.tile([P, P], F32)
+        make_identity(nc, ident_f32[:])
+        ident_bf = keep.tile([P, P], BF16)
+        make_identity(nc, ident_bf[:])
+        ones = keep.tile([P, P], BF16)
+        nc.gpsimd.memset(ones[:], 1.0)
+        eps_col = keep.tile([P, 1], F32)
+        nc.gpsimd.memset(eps_col[:], EPS)
+        warm = keep.tile([P, 1], F32)
+        nc.scalar.activation(out=warm[:], in_=eps_col[:], func=ACT.Sqrt)
+
+        wm_codes, wm_scales = quantise_weight(nc, wstage, keep, wm_raw, "wm")
+
+        transpose_attn(0)
+        quantise_attn(0)
+        vec_t = psum_x2.tile([P, P], BF16, tag="x2")
+        nc.tensor.transpose(out=vec_t[:], in_=vec_rows[:], identity=ident_bf[:])
+        vec = keep.tile([P, 12], F32)
+        nc.vector.tensor_copy(out=vec[:], in_=vec_t[:, 0:12])
+        bias_m = vec[:, 0:4]
+        gamma = vec[:, 4:8]
+        beta = vec[:, 8:12]
+        transpose_x(0)
+        first_matmul(0, 0)
+        first_matmul(0, 1)
+
+        for b in range(BATCH + 1):
+            before = b - 1
+            after = b + 1
+            if b + 3 < BATCH:
+                load_batch(b + 3)
+            if b < BATCH:
+                stats_begin(b)
+            if b == 0:
+                w1_codes, w1_scales = quantise_weight(nc, wstage, keep, w1_raw, "w1")
+                b1_ps = psum_mm.tile([P, FEATS], F32, tag="mm")
+                nc.tensor.matmul(out=b1_ps[:], lhsT=ones[:], rhs=b1_row[:], start=True, stop=True)
+                b1_all = keep.tile([P, FEATS], F32)
+                nc.vector.tensor_copy(out=b1_all[:], in_=b1_ps[:])
+            if before >= 0:
+                second_matmul(before, 0)
+            if after < BATCH:
+                transpose_attn(after)
+            if before >= 0:
+                second_matmul(before, 1)
+                second_out(before, 0)
+                second_out(before, 1)
+            if after < BATCH:
+                transpose_x(after)
+            if b < BATCH:
+                stats_end(b)
+                norm(b)
+                x2_first = outs.tile([P, HALF_TILES, FEATS], F32, name="x2_out")
+                x2_second = outs.tile([P, HALF_TILES, FEATS], F32, name="x2_out")
+            if after < BATCH:
+                quantise_attn(after)
+                first_matmul(after, 0)
+            if b < BATCH:
+                x2_tiles(b, x2_first, 0, range(0, 2))
+            if after < BATCH:
+                first_matmul(after, 1)
+            if b < BATCH:
+                x2_tiles(b, x2_first, 0, range(2, HALF_TILES))
+                store_half(out_0, b, 0, x2_first)
+                x2_tiles(b, x2_second, 1, range(HALF_TILES))
+                store_half(out_0, b, 1, x2_second)

@@ -51,7 +51,6 @@ def tile_attentionblock_pc_t_kernel(
         tc.psum_pool(name="psum_tr", bufs=2) as psum_tr,
         tc.psum_pool(name="psum_mm", bufs=4) as psum_mm,
         tc.psum_pool(name="psum_x2", bufs=2) as psum_x2,
-        tc.manual_schedule(),
     ):
         attn_sb = {}
         x_sb = {}
@@ -59,6 +58,7 @@ def tile_attentionblock_pc_t_kernel(
         x2T = {}
         sums = {}
         neg_mean = {}
+        ssq = {}
         std = {}
         gain = {}
         shift = {}
@@ -125,10 +125,14 @@ def tile_attentionblock_pc_t_kernel(
             x2T[b] = x2_t
             sums_b = small.tile([P, PACK, 2], F32, name="sums")
             sums[b] = sums_b
+            nm = small.tile([P, PACK], F32, name="neg_mean")
+            neg_mean[b] = nm
+            ssq_b = small.tile([P, PACK], F32, name="ssq")
+            ssq[b] = ssq_b
 
-        def first_matmul(b, h):
-            cols = slice(h * HALF, (h + 1) * HALF)
-            for t in range(PACK):
+        def first_matmul(b, t):
+            for h in range(2):
+                cols = slice(h * HALF, (h + 1) * HALF)
                 y_ps = psum_mm.tile([P, HALF], F32, tag="mm")
                 nc.tensor.matmul_mx(
                     out=y_ps[:],
@@ -148,30 +152,30 @@ def tile_attentionblock_pc_t_kernel(
                     op1=ADD,
                     accum_out=sums[b][:, t, h : h + 1],
                 )
-
-        def stats_begin(b):
-            nm = small.tile([P, PACK], F32, name="neg_mean")
-            neg_mean[b] = nm
-            nc.vector.tensor_tensor(out=nm[:], in0=sums[b][:, :, 0], in1=sums[b][:, :, 1], op=ADD)
-            nc.vector.tensor_scalar_mul(out=nm[:], in0=nm[:], scalar1=-1.0 / TOKENS)
-            ssq = small.tile([P, PACK], F32, name="ssq")
-            for t in range(PACK):
-                squares = feat.tile([P, TOKENS], BF16, name="squares")
-                nc.scalar.activation(
-                    out=squares[:],
-                    in_=x2T[b][:, t, :],
-                    func=ACT.Square,
-                    bias=nm[:, t : t + 1],
-                    scale=1.0,
-                    accum_out=ssq[:, t : t + 1],
-                )
-            sd = small.tile([P, PACK], F32, name="std")
-            std[b] = sd
+            nc.vector.scalar_tensor_tensor(
+                out=neg_mean[b][:, t : t + 1],
+                in0=sums[b][:, t, 0:1],
+                scalar=sums[b][:, t, 1:2],
+                in1=neg_inv_tokens[:],
+                op0=ADD,
+                op1=MULT,
+            )
+            squares = feat.tile([P, TOKENS], BF16, name="squares")
             nc.scalar.activation(
-                out=sd[:], in_=ssq[:], func=ACT.Sqrt, bias=eps_col[:], scale=1.0 / TOKENS
+                out=squares[:],
+                in_=x2T[b][:, t, :],
+                func=ACT.Square,
+                bias=neg_mean[b][:, t : t + 1],
+                scale=1.0,
+                accum_out=ssq[b][:, t : t + 1],
             )
 
         def stats_end(b):
+            sd = small.tile([P, PACK], F32, name="std")
+            std[b] = sd
+            nc.scalar.activation(
+                out=sd[:], in_=ssq[b][:], func=ACT.Sqrt, bias=eps_col[:], scale=1.0 / TOKENS
+            )
             g = small.tile([P, PACK], F32, name="gain")
             gain[b] = g
             nc.vector.reciprocal(out=g[:], in_=std[b][:])
@@ -273,6 +277,8 @@ def tile_attentionblock_pc_t_kernel(
         nc.gpsimd.memset(ones[:], 1.0)
         eps_col = keep.tile([P, 1], F32)
         nc.gpsimd.memset(eps_col[:], EPS)
+        neg_inv_tokens = keep.tile([P, 1], F32)
+        nc.gpsimd.memset(neg_inv_tokens[:], -1.0 / TOKENS)
         warm = keep.tile([P, 1], F32)
         nc.scalar.activation(out=warm[:], in_=eps_col[:], func=ACT.Sqrt)
 
@@ -288,8 +294,6 @@ def tile_attentionblock_pc_t_kernel(
         gamma = vec[:, 4:8]
         beta = vec[:, 8:12]
         transpose_x(0)
-        first_matmul(0, 0)
-        first_matmul(0, 1)
 
         for b in range(BATCH + 1):
             before = b - 1
@@ -297,7 +301,10 @@ def tile_attentionblock_pc_t_kernel(
             if b + 3 < BATCH:
                 load_batch(b + 3)
             if b < BATCH:
-                stats_begin(b)
+                for t in range(PACK):
+                    first_matmul(b, t)
+                stats_end(b)
+                norm(b)
             if b == 0:
                 w1_codes, w1_scales = quantise_weight(nc, wstage, keep, w1_raw, "w1")
                 b1_ps = psum_mm.tile([P, FEATS], F32, tag="mm")
@@ -306,28 +313,15 @@ def tile_attentionblock_pc_t_kernel(
                 nc.vector.tensor_copy(out=b1_all[:], in_=b1_ps[:])
             if before >= 0:
                 second_matmul(before, 0)
-            if after < BATCH:
-                transpose_attn(after)
-            if before >= 0:
                 second_matmul(before, 1)
                 second_out(before, 0)
                 second_out(before, 1)
             if after < BATCH:
+                transpose_attn(after)
+                quantise_attn(after)
                 transpose_x(after)
             if b < BATCH:
-                stats_end(b)
-                norm(b)
-                x2_first = outs.tile([P, HALF_TILES, FEATS], F32, name="x2_out")
-                x2_second = outs.tile([P, HALF_TILES, FEATS], F32, name="x2_out")
-            if after < BATCH:
-                quantise_attn(after)
-                first_matmul(after, 0)
-            if b < BATCH:
-                x2_tiles(b, x2_first, 0, range(0, 2))
-            if after < BATCH:
-                first_matmul(after, 1)
-            if b < BATCH:
-                x2_tiles(b, x2_first, 0, range(2, HALF_TILES))
-                store_half(out_0, b, 0, x2_first)
-                x2_tiles(b, x2_second, 1, range(HALF_TILES))
-                store_half(out_0, b, 1, x2_second)
+                for h in range(2):
+                    x2_out = outs.tile([P, HALF_TILES, FEATS], F32, name="x2_out")
+                    x2_tiles(b, x2_out, h, range(HALF_TILES))
+                    store_half(out_0, b, h, x2_out)

@@ -8,6 +8,7 @@ U8 = mybir.dt.uint8
 FP8X4 = mybir.dt.float8_e4m3fn_x4
 ADD = mybir.AluOpType.add
 MULT = mybir.AluOpType.mult
+POW = mybir.AluOpType.pow
 ACT = mybir.ActivationFunctionType
 
 P = 128
@@ -19,13 +20,17 @@ TILES = TOKENS // P
 HALF_TILES = TILES // 2
 HALF = HALF_TILES * P
 EPS = 1e-5
+RUN = 4
 
 FLOPS = 2 * 2 * BATCH * TOKENS * FEATS * FEATS
 
 
 def quantise_weight(nc, stage, keep, raw, label):
     grouped = stage.tile([P, FEATS, PACK], BF16, align_bytes=64, name="grouped_" + label)
-    nc.vector.tensor_copy(out=grouped[:], in_=raw[:].rearrange("p t c -> p c t"))
+    nc.vector.tensor_copy(
+        out=grouped[:].rearrange("p (c i) t -> p c t i", i=RUN),
+        in_=raw[:].rearrange("p t (c i) -> p c t i", i=RUN),
+    )
     codes = keep.tile([P, FEATS], U32, align_bytes=64, name="codes_" + label)
     scales = keep.tile([P, FEATS], U8, align_bytes=64, name="scales_" + label)
     nc.vector.quantize_mx(
@@ -59,7 +64,6 @@ def tile_attentionblock_pc_t_kernel(
         sums = {}
         neg_mean = {}
         ssq = {}
-        std = {}
         gain = {}
         shift = {}
         xn = {}
@@ -152,6 +156,10 @@ def tile_attentionblock_pc_t_kernel(
                     op1=ADD,
                     accum_out=sums[b][:, t, h : h + 1],
                 )
+                if h == 0 and t > 0:
+                    squared_distances(b, t - 1)
+
+        def squared_distances(b, t):
             nc.vector.scalar_tensor_tensor(
                 out=neg_mean[b][:, t : t + 1],
                 in0=sums[b][:, t, 0:1],
@@ -171,19 +179,17 @@ def tile_attentionblock_pc_t_kernel(
             )
 
         def stats_end(b):
-            sd = small.tile([P, PACK], F32, name="std")
-            std[b] = sd
-            nc.scalar.activation(
-                out=sd[:], in_=ssq[b][:], func=ACT.Sqrt, bias=eps_col[:], scale=1.0 / TOKENS
-            )
             g = small.tile([P, PACK], F32, name="gain")
             gain[b] = g
-            nc.vector.reciprocal(out=g[:], in_=std[b][:])
-            nc.vector.tensor_tensor(out=g[:], in0=g[:], in1=gamma, op=MULT)
+            nc.gpsimd.tensor_scalar(
+                out=g[:], in0=ssq[b][:], scalar1=1.0 / TOKENS, scalar2=EPS, op0=MULT, op1=ADD
+            )
+            nc.gpsimd.tensor_tensor(out=g[:], in0=g[:], in1=minus_half[:], op=POW)
+            nc.gpsimd.tensor_tensor(out=g[:], in0=g[:], in1=gamma, op=MULT)
             sh = small.tile([P, PACK], F32, name="shift")
             shift[b] = sh
-            nc.vector.tensor_tensor(out=sh[:], in0=neg_mean[b][:], in1=g[:], op=MULT)
-            nc.vector.tensor_tensor(out=sh[:], in0=sh[:], in1=beta, op=ADD)
+            nc.gpsimd.tensor_tensor(out=sh[:], in0=neg_mean[b][:], in1=g[:], op=MULT)
+            nc.gpsimd.tensor_tensor(out=sh[:], in0=sh[:], in1=beta, op=ADD)
 
         def norm(b):
             xn_b = feat.tile([P, PACK, TOKENS], BF16, name="xn")
@@ -216,26 +222,36 @@ def tile_attentionblock_pc_t_kernel(
             view = dram[b].rearrange("(p i) f -> p i f", i=TILES)
             nc.sync.dma_start(out=view[:, h * HALF_TILES : (h + 1) * HALF_TILES, :], in_=tile_sb[:])
 
+        def second_quantise(b):
+            grouped = {}
+            for h in range(2):
+                n_grouped = mx.tile([P, HALF, PACK], BF16, align_bytes=64, name="n_grouped")
+                grouped[h] = n_grouped
+                nc.vector.tensor_copy(
+                    out=n_grouped[:].rearrange("p (c i) t -> p c t i", i=RUN),
+                    in_=xn[b][:, :, h * HALF : (h + 1) * HALF].rearrange(
+                        "p t (c i) -> p c t i", i=RUN
+                    ),
+                )
+            for h in range(2):
+                codes = mx.tile([P, HALF], U32, align_bytes=64, name="n_codes")
+                scales = mx.tile([P, HALF], U8, align_bytes=64, name="n_scales")
+                n_codes[b, h] = codes
+                n_scales[b, h] = scales
+                nc.vector.quantize_mx(
+                    out=codes[:].bitcast(FP8X4),
+                    scales=scales[:],
+                    in_=grouped[h][:].rearrange("p r t -> p (r t)"),
+                )
+
         def second_matmul(b, h):
-            n_grouped = mx.tile([P, HALF, PACK], BF16, align_bytes=64, name="n_grouped")
-            nc.vector.tensor_copy(
-                out=n_grouped[:],
-                in_=xn[b][:, :, h * HALF : (h + 1) * HALF].rearrange("p t r -> p r t"),
-            )
-            codes = mx.tile([P, HALF], U32, align_bytes=64, name="n_codes")
-            scales = mx.tile([P, HALF], U8, align_bytes=64, name="n_scales")
-            nc.vector.quantize_mx(
-                out=codes[:].bitcast(FP8X4),
-                scales=scales[:],
-                in_=n_grouped[:].rearrange("p r t -> p (r t)"),
-            )
             for j in range(HALF_TILES):
                 ps = psum_mm.tile([P, FEATS], F32, tag="mm", name="ff_ps")
                 ff_ps[b, h, j] = ps
                 nc.tensor.matmul_mx(
                     out=ps[:],
-                    lhsT=codes[:, j * P : (j + 1) * P].bitcast(FP8X4),
-                    lhsT_scale=scales[:, j * P : (j + 1) * P],
+                    lhsT=n_codes[b, h][:, j * P : (j + 1) * P].bitcast(FP8X4),
+                    lhsT_scale=n_scales[b, h][:, j * P : (j + 1) * P],
                     rhs=w1_codes[:].bitcast(FP8X4),
                     rhs_scale=w1_scales[:],
                     start=True,
@@ -275,12 +291,10 @@ def tile_attentionblock_pc_t_kernel(
         make_identity(nc, ident_bf[:])
         ones = keep.tile([P, P], BF16)
         nc.gpsimd.memset(ones[:], 1.0)
-        eps_col = keep.tile([P, 1], F32)
-        nc.gpsimd.memset(eps_col[:], EPS)
+        minus_half = keep.tile([P, PACK], F32)
+        nc.gpsimd.memset(minus_half[:], -0.5)
         neg_inv_tokens = keep.tile([P, 1], F32)
         nc.gpsimd.memset(neg_inv_tokens[:], -1.0 / TOKENS)
-        warm = keep.tile([P, 1], F32)
-        nc.scalar.activation(out=warm[:], in_=eps_col[:], func=ACT.Sqrt)
 
         wm_codes, wm_scales = quantise_weight(nc, wstage, keep, wm_raw, "wm")
 
@@ -303,6 +317,7 @@ def tile_attentionblock_pc_t_kernel(
             if b < BATCH:
                 for t in range(PACK):
                     first_matmul(b, t)
+                squared_distances(b, PACK - 1)
                 stats_end(b)
                 norm(b)
             if b == 0:
@@ -312,9 +327,10 @@ def tile_attentionblock_pc_t_kernel(
                 b1_all = keep.tile([P, FEATS], F32)
                 nc.vector.tensor_copy(out=b1_all[:], in_=b1_ps[:])
             if before >= 0:
+                second_quantise(before)
                 second_matmul(before, 0)
-                second_matmul(before, 1)
                 second_out(before, 0)
+                second_matmul(before, 1)
                 second_out(before, 1)
             if after < BATCH:
                 transpose_attn(after)

@@ -8,7 +8,6 @@ U8 = mybir.dt.uint8
 FP8X4 = mybir.dt.float8_e4m3fn_x4
 ADD = mybir.AluOpType.add
 MULT = mybir.AluOpType.mult
-POW = mybir.AluOpType.pow
 ACT = mybir.ActivationFunctionType
 
 P = 128
@@ -21,16 +20,26 @@ HALF_TILES = TILES // 2
 HALF = HALF_TILES * P
 EPS = 1e-5
 RUN = 4
+WORDS = FEATS // 2
 
 FLOPS = 2 * 2 * BATCH * TOKENS * FEATS * FEATS
 
 
-def quantise_weight(nc, stage, keep, raw, label):
+def quantise_weight(nc, stage, keep, raw, label, pairs_apart):
     grouped = stage.tile([P, FEATS, PACK], BF16, align_bytes=64, name="grouped_" + label)
-    nc.vector.tensor_copy(
-        out=grouped[:].rearrange("p (c i) t -> p c t i", i=RUN),
-        in_=raw[:].rearrange("p t (c i) -> p c t i", i=RUN),
-    )
+    if pairs_apart:
+        by_pair = raw[:].rearrange("p t (u m e) -> p u e m t", u=2, e=2)
+        for u in range(2):
+            for e in range(2):
+                chunk = 2 * u + e
+                nc.vector.tensor_copy(
+                    out=grouped[:, chunk * P : (chunk + 1) * P, :], in_=by_pair[:, u, e, :, :]
+                )
+    else:
+        nc.vector.tensor_copy(
+            out=grouped[:].rearrange("p (c i) t -> p c t i", i=RUN),
+            in_=raw[:].rearrange("p t (c i) -> p c t i", i=RUN),
+        )
     codes = keep.tile([P, FEATS], U32, align_bytes=64, name="codes_" + label)
     scales = keep.tile([P, FEATS], U8, align_bytes=64, name="scales_" + label)
     nc.vector.quantize_mx(
@@ -54,7 +63,7 @@ def tile_attentionblock_pc_t_kernel(
         tc.tile_pool(name="outs", bufs=3) as outs,
         tc.tile_pool(name="small", bufs=2) as small,
         tc.psum_pool(name="psum_tr", bufs=2) as psum_tr,
-        tc.psum_pool(name="psum_mm", bufs=4) as psum_mm,
+        tc.psum_pool(name="psum_mm", bufs=2) as psum_mm,
         tc.psum_pool(name="psum_x2", bufs=2) as psum_x2,
     ):
         attn_sb = {}
@@ -64,6 +73,7 @@ def tile_attentionblock_pc_t_kernel(
         sums = {}
         neg_mean = {}
         ssq = {}
+        std = {}
         gain = {}
         shift = {}
         xn = {}
@@ -77,10 +87,15 @@ def tile_attentionblock_pc_t_kernel(
         def load_batch(b):
             a_in = inputs.tile([P, TILES * FEATS], BF16, name="a_in")
             x_in = inputs.tile([P, TILES * FEATS], BF16, name="x_in")
-            nc.sync.dma_start(out=a_in[:], in_=attn_out[b].rearrange("(p i) f -> p (i f)", i=TILES))
-            nc.sync.dma_start(out=x_in[:], in_=x[b].rearrange("(p i) f -> p (i f)", i=TILES))
             attn_sb[b] = a_in
             x_sb[b] = x_in
+            width = HALF_TILES * FEATS
+            for h in range(2):
+                cols = slice(h * width, (h + 1) * width)
+                for sb, dram in ((a_in, attn_out), (x_in, x)):
+                    nc.sync.dma_start(
+                        out=sb[:, cols], in_=dram[b].rearrange("(p i) f -> p (i f)", i=TILES)[:, cols]
+                    )
 
         def transpose_attn(b):
             a32 = attn_sb[b][:].bitcast(F32)
@@ -95,7 +110,7 @@ def tile_attentionblock_pc_t_kernel(
                         for u in range(2):
                             nc.tensor.transpose(
                                 out=at_ps[:, u, j * P : (j + 1) * P],
-                                in_=a32[:, i * 256 + u * P : i * 256 + (u + 1) * P],
+                                in_=a32[:, i * WORDS + u * P : i * WORDS + (u + 1) * P],
                                 identity=ident_f32[:],
                             )
                     nc.scalar.copy(
@@ -104,17 +119,23 @@ def tile_attentionblock_pc_t_kernel(
                     )
 
         def transpose_x(b):
+            x32 = x_sb[b][:].bitcast(F32)
             x_t = feat.tile([P, PACK, TOKENS], BF16, name="xT")
             xT[b] = x_t
-            for t in range(PACK):
-                xt_ps = psum_tr.tile([P, TOKENS], BF16, tag="tr")
-                for i in range(TILES):
-                    nc.tensor.transpose(
-                        out=xt_ps[:, i * P : (i + 1) * P],
-                        in_=x_sb[b][:, i * FEATS + t * P : i * FEATS + (t + 1) * P],
-                        identity=ident_bf[:],
+            for u in range(2):
+                for h in range(2):
+                    xt_ps = psum_tr.tile([P, HALF], F32, tag="tr")
+                    for j in range(HALF_TILES):
+                        i = h * HALF_TILES + j
+                        nc.tensor.transpose(
+                            out=xt_ps[:, j * P : (j + 1) * P],
+                            in_=x32[:, i * WORDS + u * P : i * WORDS + (u + 1) * P],
+                            identity=ident_f32[:],
+                        )
+                    nc.scalar.copy(
+                        out=x_t[:, 2 * u : 2 * u + 2, h * HALF : (h + 1) * HALF],
+                        in_=xt_ps[:].bitcast(BF16).rearrange("p (r e) -> p e r", e=2),
                     )
-                nc.scalar.copy(out=x_t[:, t, :], in_=xt_ps[:])
 
         def quantise_attn(b):
             for h in range(2):
@@ -135,11 +156,10 @@ def tile_attentionblock_pc_t_kernel(
             ssq[b] = ssq_b
 
         def first_matmul(b, t):
+            y_ps = psum_mm.tile([P, 2, HALF], F32, tag="mm")
             for h in range(2):
-                cols = slice(h * HALF, (h + 1) * HALF)
-                y_ps = psum_mm.tile([P, HALF], F32, tag="mm")
                 nc.tensor.matmul_mx(
-                    out=y_ps[:],
+                    out=y_ps[:, h, :],
                     lhsT=wm_codes[:, t * P : (t + 1) * P].bitcast(FP8X4),
                     lhsT_scale=wm_scales[:, t * P : (t + 1) * P],
                     rhs=a_codes[b, h][:].bitcast(FP8X4),
@@ -147,9 +167,11 @@ def tile_attentionblock_pc_t_kernel(
                     start=True,
                     stop=True,
                 )
+            for h in range(2):
+                cols = slice(h * HALF, (h + 1) * HALF)
                 nc.vector.scalar_tensor_tensor(
                     out=x2T[b][:, t, cols],
-                    in0=y_ps[:],
+                    in0=y_ps[:, h, :],
                     scalar=bias_m[:, t : t + 1],
                     in1=xT[b][:, t, cols],
                     op0=ADD,
@@ -179,17 +201,19 @@ def tile_attentionblock_pc_t_kernel(
             )
 
         def stats_end(b):
+            sd = small.tile([P, PACK], F32, name="std")
+            std[b] = sd
+            nc.scalar.activation(
+                out=sd[:], in_=ssq[b][:], func=ACT.Sqrt, bias=eps_col[:], scale=1.0 / TOKENS
+            )
             g = small.tile([P, PACK], F32, name="gain")
             gain[b] = g
-            nc.gpsimd.tensor_scalar(
-                out=g[:], in0=ssq[b][:], scalar1=1.0 / TOKENS, scalar2=EPS, op0=MULT, op1=ADD
-            )
-            nc.gpsimd.tensor_tensor(out=g[:], in0=g[:], in1=minus_half[:], op=POW)
-            nc.gpsimd.tensor_tensor(out=g[:], in0=g[:], in1=gamma, op=MULT)
+            nc.vector.reciprocal(out=g[:], in_=std[b][:])
+            nc.vector.tensor_tensor(out=g[:], in0=g[:], in1=gamma, op=MULT)
             sh = small.tile([P, PACK], F32, name="shift")
             shift[b] = sh
-            nc.gpsimd.tensor_tensor(out=sh[:], in0=neg_mean[b][:], in1=g[:], op=MULT)
-            nc.gpsimd.tensor_tensor(out=sh[:], in0=sh[:], in1=beta, op=ADD)
+            nc.vector.tensor_tensor(out=sh[:], in0=neg_mean[b][:], in1=g[:], op=MULT)
+            nc.vector.tensor_tensor(out=sh[:], in0=sh[:], in1=beta, op=ADD)
 
         def norm(b):
             xn_b = feat.tile([P, PACK, TOKENS], BF16, name="xn")
@@ -197,7 +221,8 @@ def tile_attentionblock_pc_t_kernel(
             for h in range(2):
                 cols = slice(h * HALF, (h + 1) * HALF)
                 for t in range(PACK):
-                    nc.gpsimd.tensor_scalar(
+                    engine = nc.vector if b == BATCH - 1 and t % 2 == 1 else nc.gpsimd
+                    engine.tensor_scalar(
                         out=xn_b[:, t, cols],
                         in0=x2T[b][:, t, cols],
                         scalar1=gain[b][:, t : t + 1],
@@ -216,42 +241,36 @@ def tile_attentionblock_pc_t_kernel(
                         in_=x2T[b][:, t, i * P : (i + 1) * P],
                         identity=ident_f32[:],
                     )
-                nc.scalar.copy(out=x2_out[:, j, :], in_=x2_ps[:])
+                nc.scalar.copy(
+                    out=x2_out[:, j, :].rearrange("p (u m e) -> p u m e", u=2, e=2),
+                    in_=x2_ps[:].rearrange("p (u e m) -> p u m e", u=2, e=2),
+                )
 
         def store_half(dram, b, h, tile_sb):
             view = dram[b].rearrange("(p i) f -> p i f", i=TILES)
             nc.sync.dma_start(out=view[:, h * HALF_TILES : (h + 1) * HALF_TILES, :], in_=tile_sb[:])
 
-        def second_quantise(b):
-            grouped = {}
-            for h in range(2):
-                n_grouped = mx.tile([P, HALF, PACK], BF16, align_bytes=64, name="n_grouped")
-                grouped[h] = n_grouped
-                nc.vector.tensor_copy(
-                    out=n_grouped[:].rearrange("p (c i) t -> p c t i", i=RUN),
-                    in_=xn[b][:, :, h * HALF : (h + 1) * HALF].rearrange(
-                        "p t (c i) -> p c t i", i=RUN
-                    ),
-                )
-            for h in range(2):
-                codes = mx.tile([P, HALF], U32, align_bytes=64, name="n_codes")
-                scales = mx.tile([P, HALF], U8, align_bytes=64, name="n_scales")
-                n_codes[b, h] = codes
-                n_scales[b, h] = scales
-                nc.vector.quantize_mx(
-                    out=codes[:].bitcast(FP8X4),
-                    scales=scales[:],
-                    in_=grouped[h][:].rearrange("p r t -> p (r t)"),
-                )
-
         def second_matmul(b, h):
+            n_grouped = mx.tile([P, HALF, PACK], BF16, align_bytes=64, name="n_grouped")
+            nc.vector.tensor_copy(
+                out=n_grouped[:].rearrange("p (c i) t -> p c t i", i=RUN),
+                in_=xn[b][:, :, h * HALF : (h + 1) * HALF].rearrange("p t (c i) -> p c t i", i=RUN),
+            )
+            codes = mx.tile([P, HALF], U32, align_bytes=64, name="n_codes")
+            scales = mx.tile([P, HALF], U8, align_bytes=64, name="n_scales")
+            nc.vector.quantize_mx(
+                out=codes[:].bitcast(FP8X4),
+                scales=scales[:],
+                in_=n_grouped[:].rearrange("p r t -> p (r t)"),
+            )
             for j in range(HALF_TILES):
-                ps = psum_mm.tile([P, FEATS], F32, tag="mm", name="ff_ps")
-                ff_ps[b, h, j] = ps
+                if j % 2 == 0:
+                    ps = psum_mm.tile([P, 2, FEATS], F32, tag="mm", name="ff_ps")
+                ff_ps[b, h, j] = ps[:, j % 2, :]
                 nc.tensor.matmul_mx(
-                    out=ps[:],
-                    lhsT=n_codes[b, h][:, j * P : (j + 1) * P].bitcast(FP8X4),
-                    lhsT_scale=n_scales[b, h][:, j * P : (j + 1) * P],
+                    out=ps[:, j % 2, :],
+                    lhsT=codes[:, j * P : (j + 1) * P].bitcast(FP8X4),
+                    lhsT_scale=scales[:, j * P : (j + 1) * P],
                     rhs=w1_codes[:].bitcast(FP8X4),
                     rhs_scale=w1_scales[:],
                     start=True,
@@ -262,7 +281,7 @@ def tile_attentionblock_pc_t_kernel(
             ff_out = outs.tile([P, HALF_TILES, FEATS], F32, name="ff_out")
             for j in range(HALF_TILES):
                 nc.vector.tensor_tensor(
-                    out=ff_out[:, j, :], in0=ff_ps[b, h, j][:], in1=b1_all[:], op=ADD
+                    out=ff_out[:, j, :], in0=ff_ps[b, h, j], in1=b1_all[:], op=ADD
                 )
             store_half(out_1, b, h, ff_out)
 
@@ -271,39 +290,42 @@ def tile_attentionblock_pc_t_kernel(
             out=wm_raw[:].rearrange("q (u e) c -> q u (e c)", u=2),
             in_=W_merge.rearrange("(u q e) c -> q u (e c)", u=2, e=2),
         )
-        vec_rows = keep.tile([P, P], BF16)
+        vec_rows = keep.tile([P, 2 * P], BF16)
         b1_row = keep.tile([P, FEATS], BF16)
         w1_raw = wstage.tile([P, PACK, FEATS], BF16)
         nc.gpsimd.memset(vec_rows[:], 0.0)
         nc.gpsimd.memset(b1_row[:], 0.0)
-        nc.sync.dma_start(out=vec_rows[0:4, :], in_=b_merge.rearrange("(t p) -> t p", p=P))
-        nc.sync.dma_start(out=vec_rows[4:8, :], in_=gamma2.rearrange("a b (t p) -> (a b t) p", p=P))
-        nc.sync.dma_start(out=vec_rows[8:12, :], in_=beta2.rearrange("a b (t p) -> (a b t) p", p=P))
+        nc.sync.dma_start(out=vec_rows[0:2, :], in_=b_merge.rearrange("(u w) -> u w", u=2))
+        nc.sync.dma_start(out=vec_rows[2:4, :], in_=gamma2.rearrange("a b (u w) -> (a b u) w", u=2))
+        nc.sync.dma_start(out=vec_rows[4:6, :], in_=beta2.rearrange("a b (u w) -> (a b u) w", u=2))
         load_batch(0)
-        nc.sync.dma_start(out=w1_raw[:], in_=W1.rearrange("(t p) c -> p t c", p=P))
+        nc.sync.dma_start(
+            out=w1_raw[:].rearrange("q (u e) c -> q u (e c)", u=2),
+            in_=W1.rearrange("(u q e) c -> q u (e c)", u=2, e=2),
+        )
         nc.sync.dma_start(out=b1_row[0:1, :], in_=b1.rearrange("(o n) -> o n", o=1))
         load_batch(1)
         load_batch(2)
 
         ident_f32 = keep.tile([P, P], F32)
         make_identity(nc, ident_f32[:])
-        ident_bf = keep.tile([P, P], BF16)
-        make_identity(nc, ident_bf[:])
         ones = keep.tile([P, P], BF16)
         nc.gpsimd.memset(ones[:], 1.0)
-        minus_half = keep.tile([P, PACK], F32)
-        nc.gpsimd.memset(minus_half[:], -0.5)
+        eps_col = keep.tile([P, 1], F32)
+        nc.gpsimd.memset(eps_col[:], EPS)
         neg_inv_tokens = keep.tile([P, 1], F32)
         nc.gpsimd.memset(neg_inv_tokens[:], -1.0 / TOKENS)
+        warm = keep.tile([P, 1], F32)
+        nc.scalar.activation(out=warm[:], in_=eps_col[:], func=ACT.Sqrt)
 
-        wm_codes, wm_scales = quantise_weight(nc, wstage, keep, wm_raw, "wm")
+        wm_codes, wm_scales = quantise_weight(nc, wstage, keep, wm_raw, "wm", True)
 
         transpose_attn(0)
         quantise_attn(0)
-        vec_t = psum_x2.tile([P, P], BF16, tag="x2")
-        nc.tensor.transpose(out=vec_t[:], in_=vec_rows[:], identity=ident_bf[:])
+        vec_t = psum_x2.tile([P, P], F32, tag="x2")
+        nc.tensor.transpose(out=vec_t[:], in_=vec_rows[:].bitcast(F32), identity=ident_f32[:])
         vec = keep.tile([P, 12], F32)
-        nc.vector.tensor_copy(out=vec[:], in_=vec_t[:, 0:12])
+        nc.vector.tensor_copy(out=vec[:], in_=vec_t[:].bitcast(BF16)[:, 0:12])
         bias_m = vec[:, 0:4]
         gamma = vec[:, 4:8]
         beta = vec[:, 8:12]
@@ -321,16 +343,15 @@ def tile_attentionblock_pc_t_kernel(
                 stats_end(b)
                 norm(b)
             if b == 0:
-                w1_codes, w1_scales = quantise_weight(nc, wstage, keep, w1_raw, "w1")
-                b1_ps = psum_mm.tile([P, FEATS], F32, tag="mm")
+                w1_codes, w1_scales = quantise_weight(nc, wstage, keep, w1_raw, "w1", False)
+                b1_ps = psum_x2.tile([P, FEATS], F32, tag="x2")
                 nc.tensor.matmul(out=b1_ps[:], lhsT=ones[:], rhs=b1_row[:], start=True, stop=True)
                 b1_all = keep.tile([P, FEATS], F32)
                 nc.vector.tensor_copy(out=b1_all[:], in_=b1_ps[:])
             if before >= 0:
-                second_quantise(before)
                 second_matmul(before, 0)
-                second_out(before, 0)
                 second_matmul(before, 1)
+                second_out(before, 0)
                 second_out(before, 1)
             if after < BATCH:
                 transpose_attn(after)

@@ -22,32 +22,31 @@ EPS = 1e-5
 RUN = 4
 WORDS = FEATS // 2
 
+STORE = 2
+
 FLOPS = 2 * 2 * BATCH * TOKENS * FEATS * FEATS
 
 
-def quantise_weight(nc, stage, keep, raw, label, pairs_apart):
-    grouped = stage.tile([P, FEATS, PACK], BF16, align_bytes=64, name="grouped_" + label)
-    if pairs_apart:
-        by_pair = raw[:].rearrange("p t (u m e) -> p u e m t", u=2, e=2)
-        for u in range(2):
-            for e in range(2):
-                chunk = 2 * u + e
-                nc.vector.tensor_copy(
-                    out=grouped[:, chunk * P : (chunk + 1) * P, :], in_=by_pair[:, u, e, :, :]
-                )
-    else:
-        nc.vector.tensor_copy(
-            out=grouped[:].rearrange("p (c i) t -> p c t i", i=RUN),
-            in_=raw[:].rearrange("p t (c i) -> p c t i", i=RUN),
-        )
-    codes = keep.tile([P, FEATS], U32, align_bytes=64, name="codes_" + label)
-    scales = keep.tile([P, FEATS], U8, align_bytes=64, name="scales_" + label)
-    nc.vector.quantize_mx(
-        out=codes[:].bitcast(FP8X4),
-        scales=scales[:],
-        in_=grouped[:].rearrange("p c t -> p (c t)"),
+def group_pairs(nc, grouped, raw, u):
+    by_pair = raw[:].rearrange("p t (u m e) -> p u e m t", u=2, e=2)
+    for e in range(2):
+        chunk = 2 * u + e
+        nc.vector.tensor_copy(out=grouped[:, chunk * P : (chunk + 1) * P, :], in_=by_pair[:, u, e, :, :])
+
+
+def group_runs(nc, grouped, raw):
+    nc.vector.tensor_copy(
+        out=grouped[:].rearrange("p (c i) t -> p c t i", i=RUN),
+        in_=raw[:].rearrange("p t (c i) -> p c t i", i=RUN),
     )
-    return codes, scales
+
+
+def quantise_columns(nc, codes, scales, grouped, cols):
+    nc.vector.quantize_mx(
+        out=codes[:, cols].bitcast(FP8X4),
+        scales=scales[:, cols],
+        in_=grouped[:, cols, :].rearrange("p c t -> p (c t)"),
+    )
 
 
 def tile_attentionblock_pc_t_kernel(
@@ -57,14 +56,15 @@ def tile_attentionblock_pc_t_kernel(
     with (
         tc.tile_pool(name="keep", bufs=1) as keep,
         tc.tile_pool(name="wstage", bufs=1) as wstage,
-        tc.tile_pool(name="inputs", bufs=3) as inputs,
+        tc.tile_pool(name="inputs", bufs=4) as inputs,
         tc.tile_pool(name="feat", bufs=2) as feat,
+        tc.tile_pool(name="x2", bufs=3) as x2_pool,
         tc.tile_pool(name="mx", bufs=2) as mx,
-        tc.tile_pool(name="outs", bufs=3) as outs,
+        tc.tile_pool(name="outs", bufs=4) as outs,
         tc.tile_pool(name="small", bufs=2) as small,
-        tc.psum_pool(name="psum_tr", bufs=2) as psum_tr,
-        tc.psum_pool(name="psum_mm", bufs=2) as psum_mm,
-        tc.psum_pool(name="psum_x2", bufs=2) as psum_x2,
+        tc.psum_pool(name="psum_tr", bufs=4) as psum_tr,
+        tc.psum_pool(name="psum_mm", bufs=4) as psum_mm,
+        tc.manual_schedule(),
     ):
         attn_sb = {}
         x_sb = {}
@@ -77,111 +77,104 @@ def tile_attentionblock_pc_t_kernel(
         gain = {}
         shift = {}
         xn = {}
+        x2_out = {}
+        ff_out = {}
         a_grouped = {}
         a_codes = {}
         a_scales = {}
+        n_grouped = {}
         n_codes = {}
         n_scales = {}
+        y_ps = {}
         ff_ps = {}
 
-        def load_batch(b):
-            a_in = inputs.tile([P, TILES * FEATS], BF16, name="a_in")
-            x_in = inputs.tile([P, TILES * FEATS], BF16, name="x_in")
-            attn_sb[b] = a_in
-            x_sb[b] = x_in
+        def load(b, dram, h):
+            if h == 0 and dram is attn_out:
+                attn_sb[b] = inputs.tile([P, TILES * FEATS], BF16, name="a_in")
+            elif h == 0:
+                x_sb[b] = inputs.tile([P, TILES * FEATS], BF16, name="x_in")
+            sb = attn_sb[b] if dram is attn_out else x_sb[b]
             width = HALF_TILES * FEATS
-            for h in range(2):
-                cols = slice(h * width, (h + 1) * width)
-                for sb, dram in ((a_in, attn_out), (x_in, x)):
-                    nc.sync.dma_start(
-                        out=sb[:, cols], in_=dram[b].rearrange("(p i) f -> p (i f)", i=TILES)[:, cols]
-                    )
+            cols = slice(h * width, (h + 1) * width)
+            nc.sync.dma_start(
+                out=sb[:, cols], in_=dram[b].rearrange("(p i) f -> p (i f)", i=TILES)[:, cols]
+            )
 
-        def transpose_attn(b):
+        def transpose_attn(b, group, by_vector=False):
+            h, pair = divmod(group, HALF_TILES // 2)
             a32 = attn_sb[b][:].bitcast(F32)
-            for h in range(2):
-                grouped = mx.tile([P, HALF * PACK], BF16, align_bytes=64, name="a_grouped")
-                a_grouped[b, h] = grouped
-                a_words = grouped[:].bitcast(F32).rearrange("p (r u) -> p r u", u=2)
-                for pair in range(HALF_TILES // 2):
-                    at_ps = psum_tr.tile([P, 2, 2 * P], F32, tag="tr")
-                    for j in range(2):
-                        i = h * HALF_TILES + pair * 2 + j
-                        for u in range(2):
-                            nc.tensor.transpose(
-                                out=at_ps[:, u, j * P : (j + 1) * P],
-                                in_=a32[:, i * WORDS + u * P : i * WORDS + (u + 1) * P],
-                                identity=ident_f32[:],
-                            )
-                    nc.scalar.copy(
-                        out=a_words[:, pair * 2 * P : (pair + 1) * 2 * P, :],
-                        in_=at_ps[:].rearrange("p u r -> p r u"),
+            if pair == 0:
+                a_grouped[b, h] = mx.tile([P, HALF * PACK], BF16, align_bytes=64, name="a_grouped")
+            a_words = a_grouped[b, h][:].bitcast(F32).rearrange("p (r u) -> p r u", u=2)
+            at_ps = psum_tr.tile([P, 2, 2 * P], F32, tag="tr")
+            for j in range(2):
+                i = group * 2 + j
+                for u in range(2):
+                    nc.tensor.transpose(
+                        out=at_ps[:, u, j * P : (j + 1) * P],
+                        in_=a32[:, i * WORDS + u * P : i * WORDS + (u + 1) * P],
+                        identity=ident_f32[:],
                     )
+            (nc.vector.tensor_copy if by_vector else nc.scalar.copy)(
+                out=a_words[:, pair * 2 * P : (pair + 1) * 2 * P, :],
+                in_=at_ps[:].rearrange("p u r -> p r u"),
+            )
 
-        def transpose_x(b):
+        def transpose_x(b, u, h):
             x32 = x_sb[b][:].bitcast(F32)
-            x_t = feat.tile([P, PACK, TOKENS], BF16, name="xT")
-            xT[b] = x_t
-            for u in range(2):
-                for h in range(2):
-                    xt_ps = psum_tr.tile([P, HALF], F32, tag="tr")
-                    for j in range(HALF_TILES):
-                        i = h * HALF_TILES + j
-                        nc.tensor.transpose(
-                            out=xt_ps[:, j * P : (j + 1) * P],
-                            in_=x32[:, i * WORDS + u * P : i * WORDS + (u + 1) * P],
-                            identity=ident_f32[:],
-                        )
-                    nc.scalar.copy(
-                        out=x_t[:, 2 * u : 2 * u + 2, h * HALF : (h + 1) * HALF],
-                        in_=xt_ps[:].bitcast(BF16).rearrange("p (r e) -> p e r", e=2),
-                    )
-
-        def quantise_attn(b):
-            for h in range(2):
-                codes = mx.tile([P, HALF], U32, align_bytes=64, name="a_codes")
-                scales = mx.tile([P, HALF], U8, align_bytes=64, name="a_scales")
-                nc.vector.quantize_mx(
-                    out=codes[:].bitcast(FP8X4), scales=scales[:], in_=a_grouped[b, h][:]
+            if b not in xT:
+                xT[b] = feat.tile([P, 2, TOKENS], F32, name="xT")
+            xt_ps = psum_tr.tile([P, HALF], F32, tag="tr")
+            for j in range(HALF_TILES):
+                i = h * HALF_TILES + j
+                nc.tensor.transpose(
+                    out=xt_ps[:, j * P : (j + 1) * P],
+                    in_=x32[:, i * WORDS + u * P : i * WORDS + (u + 1) * P],
+                    identity=ident_f32[:],
                 )
-                a_codes[b, h] = codes
-                a_scales[b, h] = scales
-            x2_t = feat.tile([P, PACK, TOKENS], F32, name="x2T")
-            x2T[b] = x2_t
-            sums_b = small.tile([P, PACK, 2], F32, name="sums")
-            sums[b] = sums_b
-            nm = small.tile([P, PACK], F32, name="neg_mean")
-            neg_mean[b] = nm
-            ssq_b = small.tile([P, PACK], F32, name="ssq")
-            ssq[b] = ssq_b
+            nc.scalar.copy(out=xT[b][:, u, h * HALF : (h + 1) * HALF], in_=xt_ps[:])
 
-        def first_matmul(b, t):
-            y_ps = psum_mm.tile([P, 2, HALF], F32, tag="mm")
-            for h in range(2):
-                nc.tensor.matmul_mx(
-                    out=y_ps[:, h, :],
-                    lhsT=wm_codes[:, t * P : (t + 1) * P].bitcast(FP8X4),
-                    lhsT_scale=wm_scales[:, t * P : (t + 1) * P],
-                    rhs=a_codes[b, h][:].bitcast(FP8X4),
-                    rhs_scale=a_scales[b, h][:],
-                    start=True,
-                    stop=True,
-                )
-            for h in range(2):
-                cols = slice(h * HALF, (h + 1) * HALF)
-                nc.vector.scalar_tensor_tensor(
-                    out=x2T[b][:, t, cols],
-                    in0=y_ps[:, h, :],
-                    scalar=bias_m[:, t : t + 1],
-                    in1=xT[b][:, t, cols],
-                    op0=ADD,
-                    op1=ADD,
-                    accum_out=sums[b][:, t, h : h + 1],
-                )
-                if h == 0 and t > 0:
-                    squared_distances(b, t - 1)
+        def quantise_attn(b, h):
+            codes = mx.tile([P, HALF], U32, align_bytes=64, name="a_codes")
+            scales = mx.tile([P, HALF], U8, align_bytes=64, name="a_scales")
+            nc.vector.quantize_mx(
+                out=codes[:].bitcast(FP8X4), scales=scales[:], in_=a_grouped[b, h][:]
+            )
+            a_codes[b, h] = codes
+            a_scales[b, h] = scales
 
-        def squared_distances(b, t):
+        def first_matmul(b, t, h):
+            y_ps[b, t, h] = psum_mm.tile([P, HALF], F32, tag="mm", name="y_ps")
+            nc.tensor.matmul_mx(
+                out=y_ps[b, t, h][:],
+                lhsT=wm_codes[:, t * P : (t + 1) * P].bitcast(FP8X4),
+                lhsT_scale=wm_scales[:, t * P : (t + 1) * P],
+                rhs=a_codes[b, h][:].bitcast(FP8X4),
+                rhs_scale=a_scales[b, h][:],
+                start=True,
+                stop=True,
+            )
+
+        def residual(b, t, h):
+            if b not in x2T:
+                x2T[b] = x2_pool.tile([P, PACK, TOKENS], F32, name="x2T")
+                sums[b] = small.tile([P, PACK, 2], F32, name="sums")
+                neg_mean[b] = small.tile([P, PACK], F32, name="neg_mean")
+                ssq[b] = small.tile([P, PACK], F32, name="ssq")
+            cols = slice(h * HALF, (h + 1) * HALF)
+            u, e = divmod(t, 2)
+            x_half = xT[b][:, u, cols].bitcast(BF16).rearrange("p (r e) -> p e r", e=2)
+            nc.vector.scalar_tensor_tensor(
+                out=x2T[b][:, t, cols],
+                in0=y_ps[b, t, h][:],
+                scalar=bias_m[:, t : t + 1],
+                in1=x_half[:, e, :],
+                op0=ADD,
+                op1=ADD,
+                accum_out=sums[b][:, t, h : h + 1],
+            )
+
+        def mean(b, t):
             nc.vector.scalar_tensor_tensor(
                 out=neg_mean[b][:, t : t + 1],
                 in0=sums[b][:, t, 0:1],
@@ -190,6 +183,8 @@ def tile_attentionblock_pc_t_kernel(
                 op0=ADD,
                 op1=MULT,
             )
+
+        def squares_of(b, t):
             squares = feat.tile([P, TOKENS], BF16, name="squares")
             nc.scalar.activation(
                 out=squares[:],
@@ -200,115 +195,151 @@ def tile_attentionblock_pc_t_kernel(
                 accum_out=ssq[b][:, t : t + 1],
             )
 
-        def stats_end(b):
-            sd = small.tile([P, PACK], F32, name="std")
-            std[b] = sd
+        def std_of(b):
+            std[b] = small.tile([P, PACK], F32, name="std")
             nc.scalar.activation(
-                out=sd[:], in_=ssq[b][:], func=ACT.Sqrt, bias=eps_col[:], scale=1.0 / TOKENS
+                out=std[b][:], in_=ssq[b][:], func=ACT.Sqrt, bias=eps_col[:], scale=1.0 / TOKENS
             )
-            g = small.tile([P, PACK], F32, name="gain")
-            gain[b] = g
-            nc.vector.reciprocal(out=g[:], in_=std[b][:])
-            nc.vector.tensor_tensor(out=g[:], in0=g[:], in1=gamma, op=MULT)
-            sh = small.tile([P, PACK], F32, name="shift")
-            shift[b] = sh
-            nc.vector.tensor_tensor(out=sh[:], in0=neg_mean[b][:], in1=g[:], op=MULT)
-            nc.vector.tensor_tensor(out=sh[:], in0=sh[:], in1=beta, op=ADD)
 
-        def norm(b):
-            xn_b = feat.tile([P, PACK, TOKENS], BF16, name="xn")
-            xn[b] = xn_b
-            for h in range(2):
-                cols = slice(h * HALF, (h + 1) * HALF)
-                for t in range(PACK):
-                    engine = nc.vector if b == BATCH - 1 and t % 2 == 1 else nc.gpsimd
-                    engine.tensor_scalar(
-                        out=xn_b[:, t, cols],
-                        in0=x2T[b][:, t, cols],
-                        scalar1=gain[b][:, t : t + 1],
-                        scalar2=shift[b][:, t : t + 1],
-                        op0=MULT,
-                        op1=ADD,
-                    )
+        def affine_step(b, step):
+            if step == 0:
+                gain[b] = small.tile([P, PACK], F32, name="gain")
+                shift[b] = small.tile([P, PACK], F32, name="shift")
+                nc.vector.reciprocal(out=gain[b][:], in_=std[b][:])
+            elif step == 1:
+                nc.vector.tensor_tensor(out=gain[b][:], in0=gain[b][:], in1=gamma, op=MULT)
+            elif step == 2:
+                nc.vector.tensor_tensor(out=shift[b][:], in0=neg_mean[b][:], in1=gain[b][:], op=MULT)
+            else:
+                nc.vector.tensor_tensor(out=shift[b][:], in0=shift[b][:], in1=beta, op=ADD)
 
-        def x2_tiles(b, x2_out, h, tiles):
-            for j in tiles:
-                i = h * HALF_TILES + j
-                x2_ps = psum_x2.tile([P, FEATS], F32, tag="x2")
-                for t in range(PACK):
-                    nc.tensor.transpose(
-                        out=x2_ps[:, t * P : (t + 1) * P],
-                        in_=x2T[b][:, t, i * P : (i + 1) * P],
-                        identity=ident_f32[:],
-                    )
-                nc.scalar.copy(
-                    out=x2_out[:, j, :].rearrange("p (u m e) -> p u m e", u=2, e=2),
-                    in_=x2_ps[:].rearrange("p (u e m) -> p u m e", u=2, e=2),
+        def norm(b, t, h, engine):
+            if b not in xn:
+                xn[b] = feat.tile([P, PACK, TOKENS], BF16, name="xn")
+            cols = slice(h * HALF, (h + 1) * HALF)
+            if engine == "scalar":
+                nc.scalar.activation(
+                    out=xn[b][:, t, cols],
+                    in_=x2T[b][:, t, cols],
+                    func=ACT.Identity,
+                    bias=shift[b][:, t : t + 1],
+                    scale=gain[b][:, t : t + 1],
+                )
+            else:
+                nc.gpsimd.tensor_scalar(
+                    out=xn[b][:, t, cols],
+                    in0=x2T[b][:, t, cols],
+                    scalar1=gain[b][:, t : t + 1],
+                    scalar2=shift[b][:, t : t + 1],
+                    op0=MULT,
+                    op1=ADD,
                 )
 
-        def store_half(dram, b, h, tile_sb):
-            view = dram[b].rearrange("(p i) f -> p i f", i=TILES)
-            nc.sync.dma_start(out=view[:, h * HALF_TILES : (h + 1) * HALF_TILES, :], in_=tile_sb[:])
+        def x2_tile(b, i):
+            if i % STORE == 0:
+                x2_out[b] = outs.tile([P, STORE, FEATS], F32, name="x2_out")
+            x2_ps = psum_tr.tile([P, FEATS], F32, tag="tr")
+            for t in range(PACK):
+                nc.tensor.transpose(
+                    out=x2_ps[:, t * P : (t + 1) * P],
+                    in_=x2T[b][:, t, i * P : (i + 1) * P],
+                    identity=ident_f32[:],
+                )
+            nc.scalar.copy(
+                out=x2_out[b][:, i % STORE, :].rearrange("p (u m e) -> p u m e", u=2, e=2),
+                in_=x2_ps[:].rearrange("p (u e m) -> p u m e", u=2, e=2),
+            )
+            store(out_0, b, i, x2_out[b])
 
-        def second_matmul(b, h):
-            n_grouped = mx.tile([P, HALF, PACK], BF16, align_bytes=64, name="n_grouped")
+        def store(dram, b, i, tile_sb):
+            if i % STORE == STORE - 1:
+                view = dram[b].rearrange("(p i) f -> p i f", i=TILES)
+                nc.sync.dma_start(out=view[:, i + 1 - STORE : i + 1, :], in_=tile_sb[:])
+
+        def group_xn(b, h):
+            n_grouped[b, h] = mx.tile([P, HALF, PACK], BF16, align_bytes=64, name="n_grouped")
             nc.vector.tensor_copy(
-                out=n_grouped[:].rearrange("p (c i) t -> p c t i", i=RUN),
+                out=n_grouped[b, h][:].rearrange("p (c i) t -> p c t i", i=RUN),
                 in_=xn[b][:, :, h * HALF : (h + 1) * HALF].rearrange("p t (c i) -> p c t i", i=RUN),
             )
-            codes = mx.tile([P, HALF], U32, align_bytes=64, name="n_codes")
-            scales = mx.tile([P, HALF], U8, align_bytes=64, name="n_scales")
-            nc.vector.quantize_mx(
-                out=codes[:].bitcast(FP8X4),
-                scales=scales[:],
-                in_=n_grouped[:].rearrange("p r t -> p (r t)"),
-            )
-            for j in range(HALF_TILES):
-                if j % 2 == 0:
-                    ps = psum_mm.tile([P, 2, FEATS], F32, tag="mm", name="ff_ps")
-                ff_ps[b, h, j] = ps[:, j % 2, :]
-                nc.tensor.matmul_mx(
-                    out=ps[:, j % 2, :],
-                    lhsT=codes[:, j * P : (j + 1) * P].bitcast(FP8X4),
-                    lhsT_scale=scales[:, j * P : (j + 1) * P],
-                    rhs=w1_codes[:].bitcast(FP8X4),
-                    rhs_scale=w1_scales[:],
-                    start=True,
-                    stop=True,
-                )
 
-        def second_out(b, h):
-            ff_out = outs.tile([P, HALF_TILES, FEATS], F32, name="ff_out")
-            for j in range(HALF_TILES):
-                nc.vector.tensor_tensor(
-                    out=ff_out[:, j, :], in0=ff_ps[b, h, j], in1=b1_all[:], op=ADD
-                )
-            store_half(out_1, b, h, ff_out)
+        def quantise_xn(b, h):
+            n_codes[b, h] = mx.tile([P, HALF], U32, align_bytes=64, name="n_codes")
+            n_scales[b, h] = mx.tile([P, HALF], U8, align_bytes=64, name="n_scales")
+            nc.vector.quantize_mx(
+                out=n_codes[b, h][:].bitcast(FP8X4),
+                scales=n_scales[b, h][:],
+                in_=n_grouped[b, h][:].rearrange("p r t -> p (r t)"),
+            )
+
+        def second_matmul(b, i):
+            h, j = divmod(i, HALF_TILES)
+            ff_ps[b, i] = psum_mm.tile([P, FEATS], F32, tag="mm", name="ff_ps")
+            nc.tensor.matmul_mx(
+                out=ff_ps[b, i][:],
+                lhsT=n_codes[b, h][:, j * P : (j + 1) * P].bitcast(FP8X4),
+                lhsT_scale=n_scales[b, h][:, j * P : (j + 1) * P],
+                rhs=w1_codes[:].bitcast(FP8X4),
+                rhs_scale=w1_scales[:],
+                start=True,
+                stop=True,
+            )
+
+        def second_out(b, i):
+            if i % STORE == 0:
+                ff_out[b] = outs.tile([P, STORE, FEATS], F32, name="ff_out")
+            nc.vector.tensor_tensor(
+                out=ff_out[b][:, i % STORE, :], in0=ff_ps[b, i][:], in1=b1_all[:], op=ADD
+            )
+            store(out_1, b, i, ff_out[b])
 
         wm_raw = wstage.tile([P, PACK, FEATS], BF16)
-        nc.sync.dma_start(
-            out=wm_raw[:].rearrange("q (u e) c -> q u (e c)", u=2),
-            in_=W_merge.rearrange("(u q e) c -> q u (e c)", u=2, e=2),
-        )
+        w1_raw = wstage.tile([P, PACK, FEATS], BF16)
+        wm_grouped = wstage.tile([P, FEATS, PACK], BF16, align_bytes=64)
+        w1_grouped = wstage.tile([P, FEATS, PACK], BF16, align_bytes=64)
+        wm_codes = keep.tile([P, FEATS], U32, align_bytes=64)
+        wm_scales = keep.tile([P, FEATS], U8, align_bytes=64)
+        w1_codes = keep.tile([P, FEATS], U32, align_bytes=64)
+        w1_scales = keep.tile([P, FEATS], U8, align_bytes=64)
         vec_rows = keep.tile([P, 2 * P], BF16)
         b1_row = keep.tile([P, FEATS], BF16)
-        w1_raw = wstage.tile([P, PACK, FEATS], BF16)
+        ident_f32 = keep.tile([P, P], F32)
         nc.gpsimd.memset(vec_rows[:], 0.0)
+        make_identity(nc, ident_f32[:])
         nc.gpsimd.memset(b1_row[:], 0.0)
+
+        def load_wm(half):
+            cols = slice(half * 2 * P, (half + 1) * 2 * P)
+            for u in range(2):
+                nc.sync.dma_start(
+                    out=wm_raw[:, 2 * u : 2 * u + 2, cols],
+                    in_=W_merge.rearrange("(u q e) c -> u q e c", u=2, e=2)[u, :, :, cols],
+                )
+
+        load_wm(0)
+        load(0, attn_out, 0)
+        load_wm(1)
+        load(0, x, 0)
         nc.sync.dma_start(out=vec_rows[0:2, :], in_=b_merge.rearrange("(u w) -> u w", u=2))
         nc.sync.dma_start(out=vec_rows[2:4, :], in_=gamma2.rearrange("a b (u w) -> (a b u) w", u=2))
         nc.sync.dma_start(out=vec_rows[4:6, :], in_=beta2.rearrange("a b (u w) -> (a b u) w", u=2))
-        load_batch(0)
+        load(0, attn_out, 1)
+        load(0, x, 1)
+        load(1, attn_out, 0)
+        load(1, attn_out, 1)
+        load(1, x, 0)
+        load(1, x, 1)
         nc.sync.dma_start(
             out=w1_raw[:].rearrange("q (u e) c -> q u (e c)", u=2),
             in_=W1.rearrange("(u q e) c -> q u (e c)", u=2, e=2),
         )
         nc.sync.dma_start(out=b1_row[0:1, :], in_=b1.rearrange("(o n) -> o n", o=1))
-        load_batch(1)
-        load_batch(2)
+        for b in range(2, BATCH):
+            load(b, attn_out, 0)
+            load(b, attn_out, 1)
+            load(b, x, 0)
+            load(b, x, 1)
 
-        ident_f32 = keep.tile([P, P], F32)
-        make_identity(nc, ident_f32[:])
         ones = keep.tile([P, P], BF16)
         nc.gpsimd.memset(ones[:], 1.0)
         eps_col = keep.tile([P, 1], F32)
@@ -318,47 +349,154 @@ def tile_attentionblock_pc_t_kernel(
         warm = keep.tile([P, 1], F32)
         nc.scalar.activation(out=warm[:], in_=eps_col[:], func=ACT.Sqrt)
 
-        wm_codes, wm_scales = quantise_weight(nc, wstage, keep, wm_raw, "wm", True)
-
-        transpose_attn(0)
-        quantise_attn(0)
-        vec_t = psum_x2.tile([P, P], F32, tag="x2")
+        group_pairs(nc, wm_grouped, wm_raw, 0)
+        quantise_columns(nc, wm_codes, wm_scales, wm_grouped, slice(0, 2 * P))
+        transpose_attn(0, 0)
+        transpose_attn(0, 1, by_vector=True)
+        group_pairs(nc, wm_grouped, wm_raw, 1)
+        quantise_attn(0, 0)
+        quantise_columns(nc, wm_codes, wm_scales, wm_grouped, slice(2 * P, FEATS))
+        transpose_x(0, 0, 0)
+        vec_t = psum_tr.tile([P, P], F32, tag="tr")
         nc.tensor.transpose(out=vec_t[:], in_=vec_rows[:].bitcast(F32), identity=ident_f32[:])
         vec = keep.tile([P, 12], F32)
-        nc.vector.tensor_copy(out=vec[:], in_=vec_t[:].bitcast(BF16)[:, 0:12])
+        nc.scalar.copy(out=vec[:], in_=vec_t[:].bitcast(BF16)[:, 0:12])
         bias_m = vec[:, 0:4]
         gamma = vec[:, 4:8]
         beta = vec[:, 8:12]
-        transpose_x(0)
+        transpose_x(0, 1, 0)
+        b1_all = keep.tile([P, FEATS], F32)
 
-        for b in range(BATCH + 1):
-            before = b - 1
-            after = b + 1
-            if b + 3 < BATCH:
-                load_batch(b + 3)
+        def prepare_w1(part):
+            if part == 0:
+                group_runs(nc, w1_grouped, w1_raw)
+            elif part == 1:
+                quantise_columns(nc, w1_codes, w1_scales, w1_grouped, slice(0, FEATS))
+            else:
+                b1_ps = psum_tr.tile([P, FEATS], F32, tag="tr")
+                nc.tensor.matmul(out=b1_ps[:], lhsT=ones[:], rhs=b1_row[:], start=True, stop=True)
+                nc.scalar.copy(out=b1_all[:], in_=b1_ps[:])
+
+        def affine(b):
+            for k in range(4):
+                affine_step(b, k)
+
+        def squares_step(b, t):
+            mean(b, t)
+            squares_of(b, t)
+            if t == PACK - 1:
+                std_of(b)
+
+        D = "D"
+        lines = [
+            [(D, 0, 0, 0), ("A", 0, 2)],
+            [(D, 0, 1, 0), ("A", 0, 3)],
+            [(D, 0, 2, 0), ("X", 0, 0, 1)],
+            [(D, 0, 3, 0), ("X", 0, 1, 1)],
+            [("B", 0, 1), ("A", 1, 0)],
+            [(D, 0, 0, 1), ("A", 1, 1)],
+            [(D, 0, 1, 1), ("A", 1, 2), ("A", 1, 3)],
+            [(D, 0, 2, 1), ("E", 0, 0), ("X", 1, 0, 0), ("X", 1, 0, 1)],
+            [(D, 0, 3, 1), ("E", 0, 1)],
+            [("B", 1, 0), ("X", 1, 1, 0), ("X", 1, 1, 1), ("E", 0, 2)],
+            [("B", 1, 1), ("E", 0, 3)],
+        ]
+        for b in range(1, BATCH + 1):
+            first = len(lines)
             if b < BATCH:
                 for t in range(PACK):
-                    first_matmul(b, t)
-                squared_distances(b, PACK - 1)
-                stats_end(b)
-                norm(b)
-            if b == 0:
-                w1_codes, w1_scales = quantise_weight(nc, wstage, keep, w1_raw, "w1", False)
-                b1_ps = psum_x2.tile([P, FEATS], F32, tag="x2")
-                nc.tensor.matmul(out=b1_ps[:], lhsT=ones[:], rhs=b1_row[:], start=True, stop=True)
-                b1_all = keep.tile([P, FEATS], F32)
-                nc.vector.tensor_copy(out=b1_all[:], in_=b1_ps[:])
-            if before >= 0:
-                second_matmul(before, 0)
-                second_matmul(before, 1)
-                second_out(before, 0)
-                second_out(before, 1)
-            if after < BATCH:
-                transpose_attn(after)
-                quantise_attn(after)
-                transpose_x(after)
-            if b < BATCH:
-                for h in range(2):
-                    x2_out = outs.tile([P, HALF_TILES, FEATS], F32, name="x2_out")
-                    x2_tiles(b, x2_out, h, range(HALF_TILES))
-                    store_half(out_0, b, h, x2_out)
+                    for h in range(2):
+                        lines.append([("D", b, t, h)])
+                if b > 1:
+                    lines[first] += [("F", b - 1, 2, 1, "gpsimd")]
+                    lines[first + 1] += [("F", b - 1, 3, 1, "gpsimd")]
+            if b == 1:
+                lines[first + 3] += [("A", 2, 0)]
+                lines[first + 4] += [("A", 2, 1)]
+                lines[first + 5] += [("A", 2, 2)]
+                lines[first + 6] += [("A", 2, 3)]
+                lines[first + 7] += [("E", 1, 0)]
+                lines += [
+                    [("W", 0), ("E", 1, 1)],
+                    [("N", 0), ("W", 1), ("W", 2)],
+                    [("F", 0, 0, 0, "gpsimd"), ("F", 0, 1, 0, "gpsimd"), ("B", 2, 0), ("E", 1, 2)],
+                    [("F", 0, 2, 0, "gpsimd"), ("F", 0, 3, 0, "gpsimd"), ("B", 2, 1), ("X", 2, 0, 0)],
+                    [("G", 0, 0), ("E", 1, 3), ("X", 2, 0, 1), ("F", 0, 0, 1, "gpsimd"), ("F", 0, 1, 1, "gpsimd")],
+                    [("H", 0, 0), ("X", 2, 1, 0), ("F", 0, 2, 1, "gpsimd"), ("F", 0, 3, 1, "gpsimd")],
+                    [("G", 0, 1), ("X", 2, 1, 1)],
+                    [("J", 0, 0)],
+                    [("H", 0, 1), ("J", 0, 1)],
+                ]
+            else:
+                if b < BATCH:
+                    lines[first + 2] += [("E", b, 0)]
+                    lines[first + 4] += [("E", b, 1)]
+                    lines[first + 6] += [("E", b, 2)]
+                if b + 1 < BATCH:
+                    lines[first] += [("A", b + 1, 0)]
+                    lines[first + 1] += [("A", b + 1, 1)]
+                    lines[first + 3] += [("A", b + 1, 2)]
+                    lines[first + 5] += [("A", b + 1, 3)]
+                    lines[first + 7] += [("X", b + 1, 0, 0)]
+                lines.append([("G", b - 1, 0)] + ([("E", b, 3)] if b < BATCH else []))
+                lines.append([("G", b - 1, 1)])
+                lines.append([("H", b - 1, 0)])
+                lines.append([("H", b - 1, 1)])
+                if b + 1 < BATCH:
+                    lines[-3] += [("X", b + 1, 0, 1)]
+                    lines[-2] += [("X", b + 1, 1, 0)]
+                    lines[-1] += [("X", b + 1, 1, 1)]
+                    lines += [[("B", b + 1, 0)], [("B", b + 1, 1)]]
+            for i in range(TILES):
+                lines.append([("I", b - 1, i)])
+                if i == 0 and b < BATCH:
+                    lines[-1] += [("N", b)]
+                if b < BATCH - 1 and 2 <= i:
+                    lines[-1] += [("F", b, (i - 2) % PACK, (i - 2) // PACK, "gpsimd")]
+                if b == BATCH - 1 and 2 <= i < 6:
+                    lines[-1] += [("F", b, (i % 2) * 2, (i - 2) // 2, "gpsimd"), ("F", b, (i % 2) * 2 + 1, (i - 2) // 2, "scalar")]
+                if b == 1 and i + 2 < TILES:
+                    lines[-1] += [("J", b - 1, i + 2)]
+                if 1 < b < BATCH:
+                    lines[-1] += [("J", b - 1, i)]
+                if b == BATCH - 1 and i % 2:
+                    lines[-1] += [("J", b, i // 2)]
+                if b == BATCH and i < 4:
+                    lines[-1] += [("J", b - 1, i + 4)]
+
+        drains = [s for line in lines for s in line if s[0] in ("D", "I")]
+        state = [0, 0]
+
+        def matmuls_ahead():
+            while state[0] < len(drains) and state[0] < state[1] + 4:
+                s = drains[state[0]]
+                if s[0] == "D":
+                    if (s[1], s[3]) not in a_codes:
+                        return
+                    first_matmul(*s[1:])
+                else:
+                    if (s[1], s[2] // HALF_TILES) not in n_codes:
+                        return
+                    second_matmul(*s[1:])
+                state[0] += 1
+
+        does = {
+            "A": transpose_attn,
+            "X": transpose_x,
+            "B": quantise_attn,
+            "D": residual,
+            "E": squares_step,
+            "N": affine,
+            "F": norm,
+            "G": group_xn,
+            "H": quantise_xn,
+            "I": second_out,
+            "J": x2_tile,
+            "W": prepare_w1,
+        }
+        for line in lines:
+            matmuls_ahead()
+            for s in line:
+                does[s[0]](*s[1:])
+                if s[0] in ("D", "I"):
+                    state[1] += 1

@@ -24,6 +24,8 @@ WORDS = FEATS // 2
 
 STORE = 2
 
+RING = 4
+
 FLOPS = 2 * 2 * BATCH * TOKENS * FEATS * FEATS
 
 
@@ -35,9 +37,13 @@ def group_pairs(nc, grouped, raw, u):
 
 
 def group_runs(nc, grouped, raw):
-    nc.vector.tensor_copy(
+    nc.gpsimd.tensor_scalar(
         out=grouped[:].rearrange("p (c i) t -> p c t i", i=RUN),
-        in_=raw[:].rearrange("p t (c i) -> p c t i", i=RUN),
+        in0=raw[:].rearrange("p t (c i) -> p c t i", i=RUN),
+        scalar1=1.0,
+        scalar2=0.0,
+        op0=MULT,
+        op1=ADD,
     )
 
 
@@ -86,6 +92,7 @@ def tile_attentionblock_pc_t_kernel(
         n_codes = {}
         n_scales = {}
         y_ps = {}
+        tr_ps = {}
         ff_ps = {}
 
         def load(b, dram, h):
@@ -100,12 +107,8 @@ def tile_attentionblock_pc_t_kernel(
                 out=sb[:, cols], in_=dram[b].rearrange("(p i) f -> p (i f)", i=TILES)[:, cols]
             )
 
-        def transpose_attn(b, group, by_vector=False):
-            h, pair = divmod(group, HALF_TILES // 2)
+        def transpose_attn(b, group):
             a32 = attn_sb[b][:].bitcast(F32)
-            if pair == 0:
-                a_grouped[b, h] = mx.tile([P, HALF * PACK], BF16, align_bytes=64, name="a_grouped")
-            a_words = a_grouped[b, h][:].bitcast(F32).rearrange("p (r u) -> p r u", u=2)
             at_ps = psum_tr.tile([P, 2, 2 * P], F32, tag="tr")
             for j in range(2):
                 i = group * 2 + j
@@ -115,6 +118,14 @@ def tile_attentionblock_pc_t_kernel(
                         in_=a32[:, i * WORDS + u * P : i * WORDS + (u + 1) * P],
                         identity=ident_f32[:],
                     )
+            tr_ps["A", b, group] = at_ps
+
+        def evict_attn(b, group, by_vector=False):
+            h, pair = divmod(group, HALF_TILES // 2)
+            if pair == 0:
+                a_grouped[b, h] = mx.tile([P, HALF * PACK], BF16, align_bytes=64, name="a_grouped")
+            a_words = a_grouped[b, h][:].bitcast(F32).rearrange("p (r u) -> p r u", u=2)
+            at_ps = tr_ps["A", b, group]
             (nc.vector.tensor_copy if by_vector else nc.scalar.copy)(
                 out=a_words[:, pair * 2 * P : (pair + 1) * 2 * P, :],
                 in_=at_ps[:].rearrange("p u r -> p r u"),
@@ -122,8 +133,6 @@ def tile_attentionblock_pc_t_kernel(
 
         def transpose_x(b, u, h):
             x32 = x_sb[b][:].bitcast(F32)
-            if b not in xT:
-                xT[b] = feat.tile([P, 2, TOKENS], F32, name="xT")
             xt_ps = psum_tr.tile([P, HALF], F32, tag="tr")
             for j in range(HALF_TILES):
                 i = h * HALF_TILES + j
@@ -132,7 +141,15 @@ def tile_attentionblock_pc_t_kernel(
                     in_=x32[:, i * WORDS + u * P : i * WORDS + (u + 1) * P],
                     identity=ident_f32[:],
                 )
-            nc.scalar.copy(out=xT[b][:, u, h * HALF : (h + 1) * HALF], in_=xt_ps[:])
+            tr_ps["X", b, u, h] = xt_ps
+
+        def evict_x(b, u, h, by_vector=False):
+            if b not in xT:
+                xT[b] = feat.tile([P, 2, TOKENS], F32, name="xT")
+            xt_ps = tr_ps["X", b, u, h]
+            (nc.vector.tensor_copy if by_vector else nc.scalar.copy)(
+                out=xT[b][:, u, h * HALF : (h + 1) * HALF], in_=xt_ps[:]
+            )
 
         def quantise_attn(b, h):
             codes = mx.tile([P, HALF], U32, align_bytes=64, name="a_codes")
@@ -226,7 +243,7 @@ def tile_attentionblock_pc_t_kernel(
                     scale=gain[b][:, t : t + 1],
                 )
             else:
-                nc.gpsimd.tensor_scalar(
+                (nc.vector if engine == "vector" else nc.gpsimd).tensor_scalar(
                     out=xn[b][:, t, cols],
                     in0=x2T[b][:, t, cols],
                     scalar1=gain[b][:, t : t + 1],
@@ -235,9 +252,7 @@ def tile_attentionblock_pc_t_kernel(
                     op1=ADD,
                 )
 
-        def x2_tile(b, i):
-            if i % STORE == 0:
-                x2_out[b] = outs.tile([P, STORE, FEATS], F32, name="x2_out")
+        def transpose_x2(b, i):
             x2_ps = psum_tr.tile([P, FEATS], F32, tag="tr")
             for t in range(PACK):
                 nc.tensor.transpose(
@@ -245,6 +260,12 @@ def tile_attentionblock_pc_t_kernel(
                     in_=x2T[b][:, t, i * P : (i + 1) * P],
                     identity=ident_f32[:],
                 )
+            tr_ps["J", b, i] = x2_ps
+
+        def evict_x2(b, i):
+            if i % STORE == 0:
+                x2_out[b] = outs.tile([P, STORE, FEATS], F32, name="x2_out")
+            x2_ps = tr_ps["J", b, i]
             nc.scalar.copy(
                 out=x2_out[b][:, i % STORE, :].rearrange("p (u m e) -> p u m e", u=2, e=2),
                 in_=x2_ps[:].rearrange("p (u e m) -> p u m e", u=2, e=2),
@@ -256,12 +277,18 @@ def tile_attentionblock_pc_t_kernel(
                 view = dram[b].rearrange("(p i) f -> p i f", i=TILES)
                 nc.sync.dma_start(out=view[:, i + 1 - STORE : i + 1, :], in_=tile_sb[:])
 
-        def group_xn(b, h):
-            n_grouped[b, h] = mx.tile([P, HALF, PACK], BF16, align_bytes=64, name="n_grouped")
-            nc.vector.tensor_copy(
-                out=n_grouped[b, h][:].rearrange("p (c i) t -> p c t i", i=RUN),
-                in_=xn[b][:, :, h * HALF : (h + 1) * HALF].rearrange("p t (c i) -> p c t i", i=RUN),
-            )
+        def group_xn(b, h, engine="vector", part=None):
+            if (b, h) not in n_grouped:
+                n_grouped[b, h] = mx.tile([P, HALF, PACK], BF16, align_bytes=64, name="n_grouped")
+            cols = slice(0, HALF) if part is None else slice(*part)
+            out = n_grouped[b, h][:, cols, :].rearrange("p (c i) t -> p c t i", i=RUN)
+            in_ = xn[b][:, :, h * HALF + cols.start : h * HALF + cols.stop].rearrange("p t (c i) -> p c t i", i=RUN)
+            if engine == "vector":
+                nc.vector.tensor_copy(out=out, in_=in_)
+            elif engine == "scalar":
+                nc.scalar.copy(out=out, in_=in_)
+            else:
+                nc.gpsimd.tensor_scalar(out=out, in0=in_, scalar1=1.0, scalar2=0.0, op0=MULT, op1=ADD)
 
         def quantise_xn(b, h):
             n_codes[b, h] = mx.tile([P, HALF], U32, align_bytes=64, name="n_codes")
@@ -352,11 +379,14 @@ def tile_attentionblock_pc_t_kernel(
         group_pairs(nc, wm_grouped, wm_raw, 0)
         quantise_columns(nc, wm_codes, wm_scales, wm_grouped, slice(0, 2 * P))
         transpose_attn(0, 0)
-        transpose_attn(0, 1, by_vector=True)
+        transpose_attn(0, 1)
+        evict_attn(0, 0)
+        evict_attn(0, 1, by_vector=True)
         group_pairs(nc, wm_grouped, wm_raw, 1)
         quantise_attn(0, 0)
         quantise_columns(nc, wm_codes, wm_scales, wm_grouped, slice(2 * P, FEATS))
         transpose_x(0, 0, 0)
+        evict_x(0, 0, 0)
         vec_t = psum_tr.tile([P, P], F32, tag="tr")
         nc.tensor.transpose(out=vec_t[:], in_=vec_rows[:].bitcast(F32), identity=ident_f32[:])
         vec = keep.tile([P, 12], F32)
@@ -365,110 +395,113 @@ def tile_attentionblock_pc_t_kernel(
         gamma = vec[:, 4:8]
         beta = vec[:, 8:12]
         transpose_x(0, 1, 0)
+        evict_x(0, 1, 0)
         b1_all = keep.tile([P, FEATS], F32)
 
         def prepare_w1(part):
             if part == 0:
                 group_runs(nc, w1_grouped, w1_raw)
-            elif part == 1:
-                quantise_columns(nc, w1_codes, w1_scales, w1_grouped, slice(0, FEATS))
             else:
-                b1_ps = psum_tr.tile([P, FEATS], F32, tag="tr")
-                nc.tensor.matmul(out=b1_ps[:], lhsT=ones[:], rhs=b1_row[:], start=True, stop=True)
-                nc.scalar.copy(out=b1_all[:], in_=b1_ps[:])
+                quantise_columns(nc, w1_codes, w1_scales, w1_grouped, slice(0, FEATS))
+
+        def spread_b1():
+            b1_ps = psum_tr.tile([P, FEATS], F32, tag="tr")
+            nc.tensor.matmul(out=b1_ps[:], lhsT=ones[:], rhs=b1_row[:], start=True, stop=True)
+            tr_ps["Z"] = b1_ps
+
+        def evict_b1():
+            nc.scalar.copy(out=b1_all[:], in_=tr_ps["Z"][:])
 
         def affine(b):
             for k in range(4):
                 affine_step(b, k)
 
         def squares_step(b, t):
-            mean(b, t)
             squares_of(b, t)
             if t == PACK - 1:
                 std_of(b)
 
-        D = "D"
-        lines = [
-            [(D, 0, 0, 0), ("A", 0, 2)],
-            [(D, 0, 1, 0), ("A", 0, 3)],
-            [(D, 0, 2, 0), ("X", 0, 0, 1)],
-            [(D, 0, 3, 0), ("X", 0, 1, 1)],
-            [("B", 0, 1), ("A", 1, 0)],
-            [(D, 0, 0, 1), ("A", 1, 1)],
-            [(D, 0, 1, 1), ("A", 1, 2), ("A", 1, 3)],
-            [(D, 0, 2, 1), ("E", 0, 0), ("X", 1, 0, 0), ("X", 1, 0, 1)],
-            [(D, 0, 3, 1), ("E", 0, 1)],
-            [("B", 1, 0), ("X", 1, 1, 0), ("X", 1, 1, 1), ("E", 0, 2)],
-            [("B", 1, 1), ("E", 0, 3)],
-        ]
-        for b in range(1, BATCH + 1):
-            first = len(lines)
-            if b < BATCH:
-                for t in range(PACK):
-                    for h in range(2):
-                        lines.append([("D", b, t, h)])
-                if b > 1:
-                    lines[first] += [("F", b - 1, 2, 1, "gpsimd")]
-                    lines[first + 1] += [("F", b - 1, 3, 1, "gpsimd")]
-            if b == 1:
-                lines[first + 3] += [("A", 2, 0)]
-                lines[first + 4] += [("A", 2, 1)]
-                lines[first + 5] += [("A", 2, 2)]
-                lines[first + 6] += [("A", 2, 3)]
-                lines[first + 7] += [("E", 1, 0)]
-                lines += [
-                    [("W", 0), ("E", 1, 1)],
-                    [("N", 0), ("W", 1), ("W", 2)],
-                    [("F", 0, 0, 0, "gpsimd"), ("F", 0, 1, 0, "gpsimd"), ("B", 2, 0), ("E", 1, 2)],
-                    [("F", 0, 2, 0, "gpsimd"), ("F", 0, 3, 0, "gpsimd"), ("B", 2, 1), ("X", 2, 0, 0)],
-                    [("G", 0, 0), ("E", 1, 3), ("X", 2, 0, 1), ("F", 0, 0, 1, "gpsimd"), ("F", 0, 1, 1, "gpsimd")],
-                    [("H", 0, 0), ("X", 2, 1, 0), ("F", 0, 2, 1, "gpsimd"), ("F", 0, 3, 1, "gpsimd")],
-                    [("G", 0, 1), ("X", 2, 1, 1)],
-                    [("J", 0, 0)],
-                    [("H", 0, 1), ("J", 0, 1)],
-                ]
-            else:
-                if b < BATCH:
-                    lines[first + 2] += [("E", b, 0)]
-                    lines[first + 4] += [("E", b, 1)]
-                    lines[first + 6] += [("E", b, 2)]
-                if b + 1 < BATCH:
-                    lines[first] += [("A", b + 1, 0)]
-                    lines[first + 1] += [("A", b + 1, 1)]
-                    lines[first + 3] += [("A", b + 1, 2)]
-                    lines[first + 5] += [("A", b + 1, 3)]
-                    lines[first + 7] += [("X", b + 1, 0, 0)]
-                lines.append([("G", b - 1, 0)] + ([("E", b, 3)] if b < BATCH else []))
-                lines.append([("G", b - 1, 1)])
-                lines.append([("H", b - 1, 0)])
-                lines.append([("H", b - 1, 1)])
-                if b + 1 < BATCH:
-                    lines[-3] += [("X", b + 1, 0, 1)]
-                    lines[-2] += [("X", b + 1, 1, 0)]
-                    lines[-1] += [("X", b + 1, 1, 1)]
-                    lines += [[("B", b + 1, 0)], [("B", b + 1, 1)]]
-            for i in range(TILES):
-                lines.append([("I", b - 1, i)])
-                if i == 0 and b < BATCH:
-                    lines[-1] += [("N", b)]
-                if b < BATCH - 1 and 2 <= i:
-                    lines[-1] += [("F", b, (i - 2) % PACK, (i - 2) // PACK, "gpsimd")]
-                if b == BATCH - 1 and 2 <= i < 6:
-                    lines[-1] += [("F", b, (i % 2) * 2, (i - 2) // 2, "gpsimd"), ("F", b, (i % 2) * 2 + 1, (i - 2) // 2, "scalar")]
-                if b == 1 and i + 2 < TILES:
-                    lines[-1] += [("J", b - 1, i + 2)]
-                if 1 < b < BATCH:
-                    lines[-1] += [("J", b - 1, i)]
-                if b == BATCH - 1 and i % 2:
-                    lines[-1] += [("J", b, i // 2)]
-                if b == BATCH and i < 4:
-                    lines[-1] += [("J", b - 1, i + 4)]
+        def adds(b):
+            entries = []
+            for t in range(PACK):
+                entries.append([("D", b, t, 0)] + ([("M", b, t - 1)] if t > 0 else []))
+                entries.append([("D", b, t, 1)])
+            return entries
 
-        drains = [s for line in lines for s in line if s[0] in ("D", "I")]
+        def one(*step):
+            return [step]
+
+        def two(*step):
+            return [[step], None]
+
+        vec = [one("D", 0, t, 0) for t in range(PACK)]
+        vec += [one("B", 0, 1), one("D", 0, 0, 1), one("D", 0, 1, 1)]
+        vec += [[("D", 0, 2, 1), ("M", 0, 0)], [("D", 0, 3, 1), ("M", 0, 1)]]
+        vec += [[("B", 1, 0), ("M", 0, 2)], [("B", 1, 1), ("M", 0, 3)]]
+        sca = [one("A", 0, 2), one("A", 0, 3), one("X", 0, 0, 1), one("X", 0, 1, 1)]
+        sca += [one("A", 1, n) for n in range(4)]
+        sca += two("E", 0, 0) + [one("X", 1, 0, 0), one("X", 1, 0, 1)] + two("E", 0, 1)
+        sca += [one("X", 1, 1, 0), one("X", 1, 1, 1)] + two("E", 0, 2) + two("E", 0, 3)
+        gps = [None] * 11 + [one("W", 0)]
+
+        vec += adds(1)
+        vec += [[("W", 1), ("M", 1, 3)], one("N", 0), None]
+        for h in range(2):
+            vec += [[("F", 0, 0, h, "vector"), ("F", 0, 1, h, "vector")], [("F", 0, 2, h, "vector"), ("F", 0, 3, h, "vector")]]
+        vec += two("G", 0, 0) + two("G", 0, 1)
+        vec += [one("H", 0, 0), one("B", 2, 0), one("H", 0, 1), one("B", 2, 1)]
+        for t in range(PACK):
+            sca += two("E", 1, t)
+        sca += [one("A", 2, n) for n in range(4)]
+        sca += [one("Z",), one("J", 0, 0), one("J", 0, 1)]
+        sca += [one("X", 2, 0, 0), one("X", 2, 0, 1), one("X", 2, 1, 0), one("X", 2, 1, 1)]
+        sca += [one("J", 0, i) for i in range(2, TILES)]
+        vec += [[("I", 0, 0), ("N", 1)]]
+        gps += [None] * (len(vec) - len(gps))
+        gps += [one("F", 1, n % PACK, 1 - n // PACK, "gpsimd") for n in range(2 * PACK)] + [one("G", 1, 1, "gpsimd")]
+        vec += [one("I", 0, i) for i in range(1, TILES)]
+
+        vec += adds(2)
+        vec += [[("H", 1, 1), ("M", 2, 3)]] + two("G", 1, 0) + [one("B", 3, 0), one("H", 1, 0), one("B", 3, 1)]
+        for t in range(PACK):
+            sca += [one("A", 3, t)] + two("E", 2, t)
+        sca += [one("J", 1, 0), one("J", 1, 1)]
+        sca += [one("X", 3, 0, 0), one("X", 3, 0, 1), one("X", 3, 1, 0), one("X", 3, 1, 1)]
+        sca += [one("J", 1, i) for i in range(2, TILES)]
+        vec += [one("I", 1, 4), one("I", 1, 5), [("I", 1, 6), ("N", 2)]]
+        gps += [None] * (len(vec) - len(gps))
+        gps += [one("F", 2, n % PACK, 1 - n // PACK, "gpsimd") for n in range(2 * PACK)] + [one("G", 2, 1, "gpsimd")]
+        vec += [one("I", 1, 7), one("I", 1, 0), one("I", 1, 1), one("I", 1, 2), one("I", 1, 3)]
+
+        vec += adds(3)
+        vec += [[("H", 2, 1), ("M", 3, 3)]] + two("G", 2, 0) + [one("H", 2, 0)]
+        for t in range(PACK):
+            sca += two("E", 3, t)
+        vec += [one("I", 2, 4), one("I", 2, 5), [("I", 2, 6), ("N", 3)], one("I", 2, 7)]
+        sca += [one("J", 2, i) for i in range(TILES)]
+        sca += [one("J", 3, i) for i in range(TILES)]
+        vec += [[("F", 3, 0, 1, "vector"), ("F", 3, 1, 1, "vector")], [("F", 3, 2, 1, "vector"), ("F", 3, 3, 1, "vector")]]
+        vec += [[("F", 3, 0, 0, "vector"), ("F", 3, 1, 0, "vector")], [("F", 3, 2, 0, "vector"), ("F", 3, 3, 0, "vector")]]
+        gps += [None] * (len(vec) - len(gps))
+        gps += [one("G", 3, 1, "gpsimd")]
+        vec += [one("I", 2, i) for i in range(4)]
+        vec += [one("H", 3, 1)] + two("G", 3, 0) + [one("H", 3, 0)]
+        vec += [one("I", 3, i) for i in (4, 5, 6, 7, 0, 1, 2, 3)]
+
+        drains = [s for entry in vec if entry for s in entry if s[0] in ("D", "I")]
+
+        rows = []
+        for n in range(max(len(vec), len(sca), len(gps))):
+            rows.append([s for queue in (vec, sca, gps) if n < len(queue) and queue[n] for s in queue[n]])
+        fills = [s for row in rows for s in row if s[0] in ("A", "X", "J", "Z")]
+        feeders = {"A": transpose_attn, "X": transpose_x, "J": transpose_x2, "Z": spread_b1}
+        fill_state = [0, 0]
         state = [0, 0]
 
         def matmuls_ahead():
-            while state[0] < len(drains) and state[0] < state[1] + 4:
+            if state[0] > state[1] + RING - 2:
+                return
+            while state[0] < len(drains) and state[0] < state[1] + RING:
                 s = drains[state[0]]
                 if s[0] == "D":
                     if (s[1], s[3]) not in a_codes:
@@ -480,23 +513,41 @@ def tile_attentionblock_pc_t_kernel(
                     second_matmul(*s[1:])
                 state[0] += 1
 
+        def transposes_ahead():
+            if fill_state[0] > fill_state[1] + RING - 2:
+                return
+            while fill_state[0] < len(fills) and fill_state[0] < fill_state[1] + RING:
+                s = fills[fill_state[0]]
+                if s[0] == "J" and (s[1], PACK - 1, 1) not in added:
+                    return
+                feeders[s[0]](*[a for a in s[1:] if a is not True])
+                fill_state[0] += 1
+
+        added = set()
         does = {
-            "A": transpose_attn,
-            "X": transpose_x,
+            "A": evict_attn,
+            "X": evict_x,
+            "Z": evict_b1,
             "B": quantise_attn,
             "D": residual,
+            "M": mean,
             "E": squares_step,
             "N": affine,
             "F": norm,
             "G": group_xn,
             "H": quantise_xn,
             "I": second_out,
-            "J": x2_tile,
+            "J": evict_x2,
             "W": prepare_w1,
         }
-        for line in lines:
+        for row in rows:
             matmuls_ahead()
-            for s in line:
+            transposes_ahead()
+            for s in row:
                 does[s[0]](*s[1:])
+                if s[0] == "D":
+                    added.add(s[1:])
                 if s[0] in ("D", "I"):
                     state[1] += 1
+                if s[0] in feeders:
+                    fill_state[1] += 1

@@ -24,6 +24,7 @@ WORDS = FEATS // 2
 
 STORE = 2
 
+LEAD = 0
 RING = 4
 
 FLOPS = 2 * 2 * BATCH * TOKENS * FEATS * FEATS
@@ -345,8 +346,8 @@ def tile_attentionblock_pc_t_kernel(
 
         load_wm(0)
         load(0, attn_out, 0)
-        load_wm(1)
         load(0, x, 0)
+        load_wm(1)
         nc.sync.dma_start(out=vec_rows[0:2, :], in_=b_merge.rearrange("(u w) -> u w", u=2))
         nc.sync.dma_start(out=vec_rows[2:4, :], in_=gamma2.rearrange("a b (u w) -> (a b u) w", u=2))
         nc.sync.dma_start(out=vec_rows[4:6, :], in_=beta2.rearrange("a b (u w) -> (a b u) w", u=2))
@@ -382,8 +383,8 @@ def tile_attentionblock_pc_t_kernel(
         transpose_attn(0, 1)
         evict_attn(0, 0)
         evict_attn(0, 1, by_vector=True)
-        group_pairs(nc, wm_grouped, wm_raw, 1)
         quantise_attn(0, 0)
+        group_pairs(nc, wm_grouped, wm_raw, 1)
         quantise_columns(nc, wm_codes, wm_scales, wm_grouped, slice(2 * P, FEATS))
         transpose_x(0, 0, 0)
         evict_x(0, 0, 0)
@@ -396,6 +397,10 @@ def tile_attentionblock_pc_t_kernel(
         beta = vec[:, 8:12]
         transpose_x(0, 1, 0)
         evict_x(0, 1, 0)
+        first_matmul(0, 0, 0)
+        first_matmul(0, 1, 0)
+        transpose_attn(0, 2)
+        transpose_attn(0, 3)
         b1_all = keep.tile([P, FEATS], F32)
 
         def prepare_w1(part):
@@ -412,9 +417,6 @@ def tile_attentionblock_pc_t_kernel(
         def evict_b1():
             nc.scalar.copy(out=b1_all[:], in_=tr_ps["Z"][:])
 
-        def affine(b):
-            for k in range(4):
-                affine_step(b, k)
 
         def squares_step(b, t):
             squares_of(b, t)
@@ -434,8 +436,8 @@ def tile_attentionblock_pc_t_kernel(
         def two(*step):
             return [[step], None]
 
-        vec = [one("D", 0, t, 0) for t in range(PACK)]
-        vec += [one("B", 0, 1), one("D", 0, 0, 1), one("D", 0, 1, 1)]
+        vec = [one("D", 0, 0, 0), one("D", 0, 1, 0), one("D", 0, 2, 0), one("B", 0, 1), one("D", 0, 3, 0)]
+        vec += [one("D", 0, 0, 1), one("D", 0, 1, 1)]
         vec += [[("D", 0, 2, 1), ("M", 0, 0)], [("D", 0, 3, 1), ("M", 0, 1)]]
         vec += [[("B", 1, 0), ("M", 0, 2)], [("B", 1, 1), ("M", 0, 3)]]
         sca = [one("A", 0, 2), one("A", 0, 3), one("X", 0, 0, 1), one("X", 0, 1, 1)]
@@ -445,7 +447,7 @@ def tile_attentionblock_pc_t_kernel(
         gps = [None] * 11 + [one("W", 0)]
 
         vec += adds(1)
-        vec += [[("W", 1), ("M", 1, 3)], one("N", 0), None]
+        vec += [[("N", 0, 0), ("M", 1, 3), ("N", 0, 1), ("W", 1), ("N", 0, 2)], [("N", 0, 3)], None]
         for h in range(2):
             vec += [[("F", 0, 0, h, "vector"), ("F", 0, 1, h, "vector")], [("F", 0, 2, h, "vector"), ("F", 0, 3, h, "vector")]]
         vec += two("G", 0, 0) + two("G", 0, 1)
@@ -456,10 +458,10 @@ def tile_attentionblock_pc_t_kernel(
         sca += [one("Z",), one("J", 0, 0), one("J", 0, 1)]
         sca += [one("X", 2, 0, 0), one("X", 2, 0, 1), one("X", 2, 1, 0), one("X", 2, 1, 1)]
         sca += [one("J", 0, i) for i in range(2, TILES)]
-        vec += [[("I", 0, 0), ("N", 1)]]
-        gps += [None] * (len(vec) - len(gps))
+        vec += [[("I", 0, 0), ("N", 1, 0)]]
+        gps += [None] * (len(vec) + 2 - len(gps))
         gps += [one("F", 1, n % PACK, 1 - n // PACK, "gpsimd") for n in range(2 * PACK)] + [one("G", 1, 1, "gpsimd")]
-        vec += [one("I", 0, i) for i in range(1, TILES)]
+        vec += [[("I", 0, 1), ("N", 1, 1)], [("I", 0, 2), ("N", 1, 2)], [("I", 0, 3), ("N", 1, 3)]] + [one("I", 0, i) for i in range(4, TILES)]
 
         vec += adds(2)
         vec += [[("H", 1, 1), ("M", 2, 3)]] + two("G", 1, 0) + [one("B", 3, 0), one("H", 1, 0), one("B", 3, 1)]
@@ -468,35 +470,29 @@ def tile_attentionblock_pc_t_kernel(
         sca += [one("J", 1, 0), one("J", 1, 1)]
         sca += [one("X", 3, 0, 0), one("X", 3, 0, 1), one("X", 3, 1, 0), one("X", 3, 1, 1)]
         sca += [one("J", 1, i) for i in range(2, TILES)]
-        vec += [one("I", 1, 4), one("I", 1, 5), [("I", 1, 6), ("N", 2)]]
-        gps += [None] * (len(vec) - len(gps))
+        vec += [one("I", 1, 4), [("I", 1, 5), ("N", 2, 0)], [("I", 1, 6), ("N", 2, 1)]]
+        gps += [None] * (len(vec) + 1 - len(gps))
         gps += [one("F", 2, n % PACK, 1 - n // PACK, "gpsimd") for n in range(2 * PACK)] + [one("G", 2, 1, "gpsimd")]
-        vec += [one("I", 1, 7), one("I", 1, 0), one("I", 1, 1), one("I", 1, 2), one("I", 1, 3)]
+        vec += [[("I", 1, 7), ("N", 2, 2)], [("I", 1, 0), ("N", 2, 3)], one("I", 1, 1), one("I", 1, 2), one("I", 1, 3)]
 
         vec += adds(3)
         vec += [[("H", 2, 1), ("M", 3, 3)]] + two("G", 2, 0) + [one("H", 2, 0)]
+        sca += [one("J", 2, i) for i in range(4)]
         for t in range(PACK):
             sca += two("E", 3, t)
-        vec += [one("I", 2, 4), one("I", 2, 5), [("I", 2, 6), ("N", 3)], one("I", 2, 7)]
-        sca += [one("J", 2, i) for i in range(TILES)]
+        vec += [one("I", 2, 4), one("I", 2, 5), one("I", 2, 6), [("I", 2, 7), ("N", 3, 0)], [("I", 2, 0), ("N", 3, 1)], [("I", 2, 1), ("N", 3, 2)], [("I", 2, 2), ("N", 3, 3)]]
+        sca += [one("J", 2, i) for i in range(4, TILES)]
         sca += [one("J", 3, i) for i in range(TILES)]
-        vec += [[("F", 3, 0, 1, "vector"), ("F", 3, 1, 1, "vector")], [("F", 3, 2, 1, "vector"), ("F", 3, 3, 1, "vector")]]
-        vec += [[("F", 3, 0, 0, "vector"), ("F", 3, 1, 0, "vector")], [("F", 3, 2, 0, "vector"), ("F", 3, 3, 0, "vector")]]
-        gps += [None] * (len(vec) - len(gps))
-        gps += [one("G", 3, 1, "gpsimd")]
-        vec += [one("I", 2, i) for i in range(4)]
-        vec += [one("H", 3, 1)] + two("G", 3, 0) + [one("H", 3, 0)]
+        vec += [[("F", 3, t, h, "vector"), ("F", 3, t + 1, h, "vector")] for h in (1, 0) for t in (0, 2)]
+        vec += two("G", 3, 1) + [one("I", 2, 3), one("H", 3, 1)] + two("G", 3, 0) + [one("H", 3, 0)]
         vec += [one("I", 3, i) for i in (4, 5, 6, 7, 0, 1, 2, 3)]
 
         drains = [s for entry in vec if entry for s in entry if s[0] in ("D", "I")]
 
-        rows = []
-        for n in range(max(len(vec), len(sca), len(gps))):
-            rows.append([s for queue in (vec, sca, gps) if n < len(queue) and queue[n] for s in queue[n]])
-        fills = [s for row in rows for s in row if s[0] in ("A", "X", "J", "Z")]
+        fills = [s for entry in sca if entry for s in entry if s[0] in ("A", "X", "J", "Z")]
         feeders = {"A": transpose_attn, "X": transpose_x, "J": transpose_x2, "Z": spread_b1}
-        fill_state = [0, 0]
-        state = [0, 0]
+        fill_state = [2, 0]
+        state = [2, 0]
 
         def matmuls_ahead():
             if state[0] > state[1] + RING - 2:
@@ -532,7 +528,7 @@ def tile_attentionblock_pc_t_kernel(
             "D": residual,
             "M": mean,
             "E": squares_step,
-            "N": affine,
+            "N": affine_step,
             "F": norm,
             "G": group_xn,
             "H": quantise_xn,
@@ -540,14 +536,56 @@ def tile_attentionblock_pc_t_kernel(
             "J": evict_x2,
             "W": prepare_w1,
         }
-        for row in rows:
-            matmuls_ahead()
-            transposes_ahead()
-            for s in row:
+        def run(entry):
+            for s in entry or []:
                 does[s[0]](*s[1:])
+                done.add(s)
                 if s[0] == "D":
                     added.add(s[1:])
                 if s[0] in ("D", "I"):
                     state[1] += 1
                 if s[0] in feeders:
                     fill_state[1] += 1
+
+        def needs(s):
+            if s[0] == "D":
+                return [("X", s[1], s[2] // 2, s[3])]
+            if s[0] == "B":
+                return [("A", s[1], 2 * s[2]), ("A", s[1], 2 * s[2] + 1)]
+            if s[0] == "N":
+                return [("E", s[1], PACK - 1)]
+            return []
+
+        def startable(entry):
+            for s in entry or []:
+                if s[0] == "E" and ("M",) + s[1:] not in done:
+                    return False
+                if s[0] == "J" and ("D", s[1], PACK - 1, 1) not in done:
+                    return False
+                if s[0] == "F" and ("N", s[1], 3) not in done:
+                    return False
+            return True
+
+        done = set()
+        sca_steps = set([s for entry in sca if entry for s in entry])
+        at = 0
+        for n in range(max(len(vec), len(gps))):
+            matmuls_ahead()
+            transposes_ahead()
+            entry = vec[n] if n < len(vec) else None
+            for s in entry or []:
+                while not all(need in done for need in needs(s) if need in sca_steps):
+                    transposes_ahead()
+                    run(sca[at])
+                    at += 1
+            run(entry)
+            matmuls_ahead()
+            while at < len(sca) and at < n + 1 + LEAD and startable(sca[at]):
+                transposes_ahead()
+                run(sca[at])
+                at += 1
+            run(gps[n] if n < len(gps) else None)
+        while at < len(sca):
+            transposes_ahead()
+            run(sca[at])
+            at += 1

@@ -31,10 +31,10 @@ FLOPS = 2 * 2 * BATCH * TOKENS * FEATS * FEATS
 
 
 def group_pairs(nc, grouped, raw, u):
-    by_pair = raw[:].rearrange("p t (u m e) -> p u e m t", u=2, e=2)
+    by_pair = raw[:].rearrange("p t (m e) -> p e m t", e=2)
     for e in range(2):
         chunk = 2 * u + e
-        nc.vector.tensor_copy(out=grouped[:, chunk * P : (chunk + 1) * P, :], in_=by_pair[:, u, e, :, :])
+        nc.vector.tensor_copy(out=grouped[:, chunk * P : (chunk + 1) * P, :], in_=by_pair[:, e, :, :])
 
 
 def group_runs(nc, grouped, raw):
@@ -67,6 +67,7 @@ def tile_attentionblock_pc_t_kernel(
         tc.tile_pool(name="feat", bufs=2) as feat,
         tc.tile_pool(name="x2", bufs=3) as x2_pool,
         tc.tile_pool(name="mx", bufs=2) as mx,
+        tc.tile_pool(name="xn", bufs=4) as xn_pool,
         tc.tile_pool(name="outs", bufs=4) as outs,
         tc.tile_pool(name="small", bufs=2) as small,
         tc.psum_pool(name="psum_tr", bufs=4) as psum_tr,
@@ -232,12 +233,12 @@ def tile_attentionblock_pc_t_kernel(
                 nc.vector.tensor_tensor(out=shift[b][:], in0=shift[b][:], in1=beta, op=ADD)
 
         def norm(b, t, h, engine):
-            if b not in xn:
-                xn[b] = feat.tile([P, PACK, TOKENS], BF16, name="xn")
+            if (b, h) not in xn:
+                xn[b, h] = xn_pool.tile([P, PACK, HALF], BF16, name="xn")
             cols = slice(h * HALF, (h + 1) * HALF)
             if engine == "scalar":
                 nc.scalar.activation(
-                    out=xn[b][:, t, cols],
+                    out=xn[b, h][:, t, :],
                     in_=x2T[b][:, t, cols],
                     func=ACT.Identity,
                     bias=shift[b][:, t : t + 1],
@@ -245,7 +246,7 @@ def tile_attentionblock_pc_t_kernel(
                 )
             else:
                 (nc.vector if engine == "vector" else nc.gpsimd).tensor_scalar(
-                    out=xn[b][:, t, cols],
+                    out=xn[b, h][:, t, :],
                     in0=x2T[b][:, t, cols],
                     scalar1=gain[b][:, t : t + 1],
                     scalar2=shift[b][:, t : t + 1],
@@ -283,7 +284,7 @@ def tile_attentionblock_pc_t_kernel(
                 n_grouped[b, h] = mx.tile([P, HALF, PACK], BF16, align_bytes=64, name="n_grouped")
             cols = slice(0, HALF) if part is None else slice(*part)
             out = n_grouped[b, h][:, cols, :].rearrange("p (c i) t -> p c t i", i=RUN)
-            in_ = xn[b][:, :, h * HALF + cols.start : h * HALF + cols.stop].rearrange("p t (c i) -> p c t i", i=RUN)
+            in_ = xn[b, h][:, :, cols].rearrange("p t (c i) -> p c t i", i=RUN)
             if engine == "vector":
                 nc.vector.tensor_copy(out=out, in_=in_)
             elif engine == "scalar":
@@ -321,7 +322,7 @@ def tile_attentionblock_pc_t_kernel(
             )
             store(out_1, b, i, ff_out[b])
 
-        wm_raw = wstage.tile([P, PACK, FEATS], BF16)
+        wm_raw = [wstage.tile([P, PACK, 2 * P], BF16, name="wm_raw0"), wstage.tile([P, PACK, 2 * P], BF16, name="wm_raw1")]
         w1_raw = wstage.tile([P, PACK, FEATS], BF16)
         wm_grouped = wstage.tile([P, FEATS, PACK], BF16, align_bytes=64)
         w1_grouped = wstage.tile([P, FEATS, PACK], BF16, align_bytes=64)
@@ -340,7 +341,7 @@ def tile_attentionblock_pc_t_kernel(
             cols = slice(half * 2 * P, (half + 1) * 2 * P)
             for u in range(2):
                 nc.sync.dma_start(
-                    out=wm_raw[:, 2 * u : 2 * u + 2, cols],
+                    out=wm_raw[half][:, 2 * u : 2 * u + 2, :],
                     in_=W_merge.rearrange("(u q e) c -> u q e c", u=2, e=2)[u, :, :, cols],
                 )
 
@@ -377,14 +378,14 @@ def tile_attentionblock_pc_t_kernel(
         warm = keep.tile([P, 1], F32)
         nc.scalar.activation(out=warm[:], in_=eps_col[:], func=ACT.Sqrt)
 
-        group_pairs(nc, wm_grouped, wm_raw, 0)
+        group_pairs(nc, wm_grouped, wm_raw[0], 0)
         quantise_columns(nc, wm_codes, wm_scales, wm_grouped, slice(0, 2 * P))
         transpose_attn(0, 0)
         transpose_attn(0, 1)
         evict_attn(0, 0)
         evict_attn(0, 1, by_vector=True)
         quantise_attn(0, 0)
-        group_pairs(nc, wm_grouped, wm_raw, 1)
+        group_pairs(nc, wm_grouped, wm_raw[1], 1)
         quantise_columns(nc, wm_codes, wm_scales, wm_grouped, slice(2 * P, FEATS))
         transpose_x(0, 0, 0)
         evict_x(0, 0, 0)

@@ -453,31 +453,30 @@ def tile_attentionblock_pc_t_kernel(
             vec += [[("F", 0, 0, h, "vector"), ("F", 0, 1, h, "vector")], [("F", 0, 2, h, "vector"), ("F", 0, 3, h, "vector")]]
         vec += two("G", 0, 0) + two("G", 0, 1)
         vec += [one("H", 0, 0), one("B", 2, 0), one("H", 0, 1), one("B", 2, 1)]
-        for t in range(PACK):
-            sca += two("E", 1, t)
-        sca += [one("A", 2, n) for n in range(4)]
-        sca += [one("Z",), one("J", 0, 0), one("J", 0, 1)]
-        sca += [one("X", 2, 0, 0), one("X", 2, 0, 1), one("X", 2, 1, 0), one("X", 2, 1, 1)]
-        sca += [one("J", 0, i) for i in range(2, TILES)]
-        vec += [[("I", 0, 0), ("N", 1, 0)]]
-        gps += [None] * (len(vec) + 2 - len(gps))
-        gps += [one("F", 1, n % PACK, 1 - n // PACK, "gpsimd") for n in range(2 * PACK)] + [one("G", 1, 1, "gpsimd")]
-        vec += [[("I", 0, 1), ("N", 1, 1)], [("I", 0, 2), ("N", 1, 2)], [("I", 0, 3), ("N", 1, 3)]] + [one("I", 0, i) for i in range(4, TILES)]
+        sca += [one("J", 0, i) for i in range(0)] + two("E", 1, 0) + two("E", 1, 1)
+        sca += [one("A", 2, n) for n in range(4)] + [one("Z",)] + [one("J", 0, i) for i in range(0, 2)]
+        sca += [one("X", 2, 0, 0), one("X", 2, 0, 1)] + two("E", 1, 2) + two("E", 1, 3)
+        sca += [one("X", 2, 1, 0), one("X", 2, 1, 1)] + [one("J", 0, i) for i in range(2, TILES)]
+        vec += [one("I", 0, n) for n in range(TILES)]
+        for k in range(4):
+            vec[len(vec) - TILES + 4 + k] += [("N", 1, k)]
+        gps += [None] * (len(vec) - TILES + 8 - len(gps))
+        gps += [one("F", 1, n % PACK, 1 - n // PACK, "gpsimd") for n in range(2 * PACK)]
 
         vec += adds(2)
-        vec += [[("H", 1, 1), ("M", 2, 3)]] + two("G", 1, 0) + [one("B", 3, 0), one("H", 1, 0), one("B", 3, 1)]
-        for t in range(PACK):
-            sca += [one("A", 3, t)] + two("E", 2, t)
-        sca += [one("J", 1, 0), one("J", 1, 1)]
-        sca += [one("X", 3, 0, 0), one("X", 3, 0, 1), one("X", 3, 1, 0), one("X", 3, 1, 1)]
+        vec += [[("G", 1, 1), ("M", 2, 3)], None] + two("G", 1, 0) + [one("H", 1, 1), one("B", 3, 0), one("H", 1, 0), one("B", 3, 1)]
+        sca += [one("A", 3, 0), one("A", 3, 1)] + two("E", 2, 0) + [one("A", 3, 2), one("A", 3, 3)] + two("E", 2, 1)
+        sca += [one("J", 1, i) for i in range(2)] + two("E", 2, 2)
+        sca += [one("X", 3, 0, 0), one("X", 3, 0, 1)] + two("E", 2, 3) + [one("X", 3, 1, 0), one("X", 3, 1, 1)]
         sca += [one("J", 1, i) for i in range(2, TILES)]
-        vec += [one("I", 1, 4), [("I", 1, 5), ("N", 2, 0)], [("I", 1, 6), ("N", 2, 1)]]
-        gps += [None] * (len(vec) + 1 - len(gps))
-        gps += [one("F", 2, n % PACK, 1 - n // PACK, "gpsimd") for n in range(2 * PACK)] + [one("G", 2, 1, "gpsimd")]
-        vec += [[("I", 1, 7), ("N", 2, 2)], [("I", 1, 0), ("N", 2, 3)], one("I", 1, 1), one("I", 1, 2), one("I", 1, 3)]
+        vec += [one("I", 1, n) for n in (4, 5, 6, 7, 0, 1, 2, 3)]
+        for k in range(4):
+            vec[len(vec) - TILES + 3 + k] += [("N", 2, k)]
+        gps += [None] * (len(vec) - TILES + 7 - len(gps))
+        gps += [one("F", 2, n % PACK, 1 - n // PACK, "gpsimd") for n in range(2 * PACK)]
 
         vec += adds(3)
-        vec += [[("H", 2, 1), ("M", 3, 3)]] + two("G", 2, 0) + [one("H", 2, 0)]
+        vec += [[("G", 2, 1), ("M", 3, 3)], None] + two("G", 2, 0) + [one("H", 2, 1), one("H", 2, 0)]
         sca += [one("J", 2, i) for i in range(4)]
         for t in range(PACK):
             sca += two("E", 3, t)

@@ -8,6 +8,7 @@ U8 = mybir.dt.uint8
 FP8X4 = mybir.dt.float8_e4m3fn_x4
 ADD = mybir.AluOpType.add
 MULT = mybir.AluOpType.mult
+POW = mybir.AluOpType.pow
 ACT = mybir.ActivationFunctionType
 
 P = 128
@@ -63,12 +64,12 @@ def tile_attentionblock_pc_t_kernel(
     with (
         tc.tile_pool(name="keep", bufs=1) as keep,
         tc.tile_pool(name="wstage", bufs=1) as wstage,
-        tc.tile_pool(name="inputs", bufs=4) as inputs,
+        tc.tile_pool(name="inputs", bufs=3) as inputs,
         tc.tile_pool(name="feat", bufs=2) as feat,
         tc.tile_pool(name="x2", bufs=3) as x2_pool,
         tc.tile_pool(name="mx", bufs=2) as mx,
         tc.tile_pool(name="xn", bufs=4) as xn_pool,
-        tc.tile_pool(name="outs", bufs=4) as outs,
+        tc.tile_pool(name="outs", bufs=6) as outs,
         tc.tile_pool(name="small", bufs=2) as small,
         tc.psum_pool(name="psum_tr", bufs=4) as psum_tr,
         tc.psum_pool(name="psum_mm", bufs=4) as psum_mm,
@@ -232,13 +233,25 @@ def tile_attentionblock_pc_t_kernel(
             else:
                 nc.vector.tensor_tensor(out=shift[b][:], in0=shift[b][:], in1=beta, op=ADD)
 
+        def affine_by_gpsimd(b):
+            gain[b] = small.tile([P, PACK], F32, name="gain")
+            shift[b] = small.tile([P, PACK], F32, name="shift")
+            g, s = gain[b][:], shift[b][:]
+            nc.gpsimd.tensor_scalar(
+                out=g, in0=ssq[b][:], scalar1=1.0 / TOKENS, scalar2=EPS, op0=MULT, op1=ADD
+            )
+            nc.gpsimd.tensor_tensor(out=g, in0=g, in1=neg_half[:], op=POW)
+            nc.gpsimd.tensor_tensor(out=g, in0=g, in1=gamma, op=MULT)
+            nc.gpsimd.tensor_tensor(out=s, in0=neg_mean[b][:], in1=g, op=MULT)
+            nc.gpsimd.tensor_tensor(out=s, in0=s, in1=beta, op=ADD)
+
         def norm(b, t, h, engine):
             if (b, h) not in xn:
-                xn[b, h] = xn_pool.tile([P, PACK, HALF], BF16, name="xn")
+                xn[b, h] = xn_pool.tile([P, 2, HALF, 2], BF16, align_bytes=64, name="xn")
             cols = slice(h * HALF, (h + 1) * HALF)
             if engine == "scalar":
                 nc.scalar.activation(
-                    out=xn[b, h][:, t, :],
+                    out=xn[b, h][:, t // 2, :, t % 2],
                     in_=x2T[b][:, t, cols],
                     func=ACT.Identity,
                     bias=shift[b][:, t : t + 1],
@@ -246,7 +259,7 @@ def tile_attentionblock_pc_t_kernel(
                 )
             else:
                 (nc.vector if engine == "vector" else nc.gpsimd).tensor_scalar(
-                    out=xn[b, h][:, t, :],
+                    out=xn[b, h][:, t // 2, :, t % 2],
                     in0=x2T[b][:, t, cols],
                     scalar1=gain[b][:, t : t + 1],
                     scalar2=shift[b][:, t : t + 1],
@@ -279,18 +292,13 @@ def tile_attentionblock_pc_t_kernel(
                 view = dram[b].rearrange("(p i) f -> p i f", i=TILES)
                 nc.sync.dma_start(out=view[:, i + 1 - STORE : i + 1, :], in_=tile_sb[:])
 
-        def group_xn(b, h, engine="vector", part=None):
-            if (b, h) not in n_grouped:
-                n_grouped[b, h] = mx.tile([P, HALF, PACK], BF16, align_bytes=64, name="n_grouped")
-            cols = slice(0, HALF) if part is None else slice(*part)
-            out = n_grouped[b, h][:, cols, :].rearrange("p (c i) t -> p c t i", i=RUN)
-            in_ = xn[b, h][:, :, cols].rearrange("p t (c i) -> p c t i", i=RUN)
-            if engine == "vector":
-                nc.vector.tensor_copy(out=out, in_=in_)
-            elif engine == "scalar":
-                nc.scalar.copy(out=out, in_=in_)
-            else:
-                nc.gpsimd.tensor_scalar(out=out, in0=in_, scalar1=1.0, scalar2=0.0, op0=MULT, op1=ADD)
+        def group_xn(b, h):
+            n_grouped[b, h] = mx.tile([P, HALF, PACK], BF16, align_bytes=64, name="n_grouped")
+            words = xn[b, h][:].rearrange("p u c e -> p (u c e)").bitcast(F32)
+            nc.vector.tensor_copy(
+                out=n_grouped[b, h][:].rearrange("p c t -> p (c t)").bitcast(F32).rearrange("p (c u) -> p c u", u=2),
+                in_=words.rearrange("p (u c) -> p c u", u=2),
+            )
 
         def quantise_xn(b, h):
             n_codes[b, h] = mx.tile([P, HALF], U32, align_bytes=64, name="n_codes")
@@ -363,16 +371,21 @@ def tile_attentionblock_pc_t_kernel(
             in_=W1.rearrange("(u q e) c -> q u (e c)", u=2, e=2),
         )
         nc.sync.dma_start(out=b1_row[0:1, :], in_=b1.rearrange("(o n) -> o n", o=1))
-        for b in range(2, BATCH):
+
+        def load_batch(b):
             load(b, attn_out, 0)
             load(b, attn_out, 1)
             load(b, x, 0)
             load(b, x, 1)
 
+        load_batch(2)
+
         ones = keep.tile([P, P], BF16)
         nc.gpsimd.memset(ones[:], 1.0)
         eps_col = keep.tile([P, 1], F32)
         nc.gpsimd.memset(eps_col[:], EPS)
+        neg_half = keep.tile([P, PACK], F32)
+        nc.gpsimd.memset(neg_half[:], -0.5)
         neg_inv_tokens = keep.tile([P, 1], F32)
         nc.gpsimd.memset(neg_inv_tokens[:], -1.0 / TOKENS)
         warm = keep.tile([P, 1], F32)
@@ -421,7 +434,7 @@ def tile_attentionblock_pc_t_kernel(
 
         def squares_step(b, t):
             squares_of(b, t)
-            if t == PACK - 1:
+            if t == PACK - 1 and b in (0, BATCH - 1):
                 std_of(b)
 
         def adds(b):
@@ -445,12 +458,12 @@ def tile_attentionblock_pc_t_kernel(
         sca += [one("A", 1, n) for n in range(4)]
         sca += two("E", 0, 0) + [one("X", 1, 0, 0), one("X", 1, 0, 1)] + two("E", 0, 1)
         sca += [one("X", 1, 1, 0), one("X", 1, 1, 1)] + two("E", 0, 2) + two("E", 0, 3)
-        gps = [None] * 11 + [one("W", 0)]
+        gps = [None] * 8 + [one("L", 3), None, None, one("W", 0)]
 
         vec += adds(1)
         vec += [[("N", 0, 0), ("M", 1, 3), ("N", 0, 1), ("W", 1), ("N", 0, 2)], [("N", 0, 3)], None]
         for h in range(2):
-            vec += [[("F", 0, 0, h, "vector"), ("F", 0, 1, h, "vector")], [("F", 0, 2, h, "vector"), ("F", 0, 3, h, "vector")]]
+            vec += [[("F", 0, 0, h, "vector"), ("F", 0, 2, h, "vector")], [("F", 0, 1, h, "vector"), ("F", 0, 3, h, "vector")]]
         vec += two("G", 0, 0) + two("G", 0, 1)
         vec += [one("H", 0, 0), one("B", 2, 0), one("H", 0, 1), one("B", 2, 1)]
         sca += [one("J", 0, i) for i in range(0)] + two("E", 1, 0) + two("E", 1, 1)
@@ -458,22 +471,18 @@ def tile_attentionblock_pc_t_kernel(
         sca += [one("X", 2, 0, 0), one("X", 2, 0, 1)] + two("E", 1, 2) + two("E", 1, 3)
         sca += [one("X", 2, 1, 0), one("X", 2, 1, 1)] + [one("J", 0, i) for i in range(2, TILES)]
         vec += [one("I", 0, n) for n in range(TILES)]
-        for k in range(4):
-            vec[len(vec) - TILES + 4 + k] += [("N", 1, k)]
-        gps += [None] * (len(vec) - TILES + 8 - len(gps))
-        gps += [one("F", 1, n % PACK, 1 - n // PACK, "gpsimd") for n in range(2 * PACK)]
+        gps += [None] * (len(vec) - TILES + 5 - len(gps)) + [one("Q", 1)]
+        gps += [one("F", 1, t, h, "gpsimd") for h in (1, 0) for t in (0, 2, 1, 3)]
 
         vec += adds(2)
         vec += [[("G", 1, 1), ("M", 2, 3)], None] + two("G", 1, 0) + [one("H", 1, 1), one("B", 3, 0), one("H", 1, 0), one("B", 3, 1)]
         sca += [one("A", 3, 0), one("A", 3, 1)] + two("E", 2, 0) + [one("A", 3, 2), one("A", 3, 3)] + two("E", 2, 1)
-        sca += [one("J", 1, i) for i in range(2)] + two("E", 2, 2)
-        sca += [one("X", 3, 0, 0), one("X", 3, 0, 1)] + two("E", 2, 3) + [one("X", 3, 1, 0), one("X", 3, 1, 1)]
+        sca += two("E", 2, 2) + [one("J", 1, i) for i in range(2)] + two("E", 2, 3) + [one("J", 1, i) for i in range(2, 2)]
+        sca += [one("X", 3, u, h) for u in range(2) for h in range(2)]
         sca += [one("J", 1, i) for i in range(2, TILES)]
         vec += [one("I", 1, n) for n in (4, 5, 6, 7, 0, 1, 2, 3)]
-        for k in range(4):
-            vec[len(vec) - TILES + 3 + k] += [("N", 2, k)]
-        gps += [None] * (len(vec) - TILES + 7 - len(gps))
-        gps += [one("F", 2, n % PACK, 1 - n // PACK, "gpsimd") for n in range(2 * PACK)]
+        gps += [None] * (len(vec) - TILES + 2 - len(gps)) + [one("Q", 2)]
+        gps += [one("F", 2, t, h, "gpsimd") for h in (1, 0) for t in (0, 2, 1, 3)]
 
         vec += adds(3)
         vec += [[("G", 2, 1), ("M", 3, 3)], None] + two("G", 2, 0) + [one("H", 2, 1), one("H", 2, 0)]
@@ -483,7 +492,7 @@ def tile_attentionblock_pc_t_kernel(
         vec += [one("I", 2, 4), one("I", 2, 5), one("I", 2, 6), [("I", 2, 7), ("N", 3, 0)], [("I", 2, 0), ("N", 3, 1)], [("I", 2, 1), ("N", 3, 2)], [("I", 2, 2), ("N", 3, 3)]]
         sca += [one("J", 2, i) for i in range(4, TILES)]
         sca += [one("J", 3, i) for i in range(TILES)]
-        vec += [[("F", 3, t, h, "vector"), ("F", 3, t + 1, h, "vector")] for h in (1, 0) for t in (0, 2)]
+        vec += [[("F", 3, t, h, "vector"), ("F", 3, t + 2, h, "vector")] for h in (1, 0) for t in (0, 1)]
         vec += two("G", 3, 1) + [one("I", 2, 3), one("H", 3, 1)] + two("G", 3, 0) + [one("H", 3, 0)]
         vec += [one("I", 3, i) for i in (4, 5, 6, 7, 0, 1, 2, 3)]
 
@@ -529,11 +538,13 @@ def tile_attentionblock_pc_t_kernel(
             "M": mean,
             "E": squares_step,
             "N": affine_step,
+            "Q": affine_by_gpsimd,
             "F": norm,
             "G": group_xn,
             "H": quantise_xn,
             "I": second_out,
             "J": evict_x2,
+            "L": load_batch,
             "W": prepare_w1,
         }
         def run(entry):
@@ -552,7 +563,7 @@ def tile_attentionblock_pc_t_kernel(
                 return [("X", s[1], s[2] // 2, s[3])]
             if s[0] == "B":
                 return [("A", s[1], 2 * s[2]), ("A", s[1], 2 * s[2] + 1)]
-            if s[0] == "N":
+            if s[0] in ("N", "Q"):
                 return [("E", s[1], PACK - 1)]
             return []
 
@@ -584,7 +595,13 @@ def tile_attentionblock_pc_t_kernel(
                 transposes_ahead()
                 run(sca[at])
                 at += 1
-            run(gps[n] if n < len(gps) else None)
+            entry = gps[n] if n < len(gps) else None
+            for s in entry or []:
+                while not all(need in done for need in needs(s) if need in sca_steps):
+                    transposes_ahead()
+                    run(sca[at])
+                    at += 1
+            run(entry)
         while at < len(sca):
             transposes_ahead()
             run(sca[at])

@@ -195,11 +195,11 @@ def tile_attentionblock_pc_t_kernel(
             )
 
         def mean(b, t):
-            nc.vector.scalar_tensor_tensor(
+            nc.vector.tensor_scalar(
                 out=neg_mean[b][:, t : t + 1],
                 in0=sums[b][:, t, 0:1],
-                scalar=sums[b][:, t, 1:2],
-                in1=neg_inv_tokens[:],
+                scalar1=sums[b][:, t, 1:2],
+                scalar2=-1.0 / TOKENS,
                 op0=ADD,
                 op1=MULT,
             )
@@ -386,8 +386,6 @@ def tile_attentionblock_pc_t_kernel(
         nc.gpsimd.memset(eps_col[:], EPS)
         neg_half = keep.tile([P, PACK], F32)
         nc.gpsimd.memset(neg_half[:], -0.5)
-        neg_inv_tokens = keep.tile([P, 1], F32)
-        nc.gpsimd.memset(neg_inv_tokens[:], -1.0 / TOKENS)
         warm = keep.tile([P, 1], F32)
         nc.scalar.activation(out=warm[:], in_=eps_col[:], func=ACT.Sqrt)
 

@@ -32,7 +32,7 @@ FLOPS = 2 * 2 * BATCH * TOKENS * FEATS * FEATS
 
 
 def group_pairs(nc, grouped, raw, u):
-    by_pair = raw[:].rearrange("p t (m e) -> p e m t", e=2)
+    by_pair = raw.rearrange("p t (m e) -> p e m t", e=2)
     for e in range(2):
         chunk = 2 * u + e
         nc.vector.tensor_copy(out=grouped[:, chunk * P : (chunk + 1) * P, :], in_=by_pair[:, e, :, :])
@@ -40,8 +40,8 @@ def group_pairs(nc, grouped, raw, u):
 
 def group_runs(nc, grouped, raw):
     nc.gpsimd.tensor_scalar(
-        out=grouped[:].rearrange("p (c i) t -> p c t i", i=RUN),
-        in0=raw[:].rearrange("p t (c i) -> p c t i", i=RUN),
+        out=grouped[:],
+        in0=raw[:].rearrange("p t c -> p c t"),
         scalar1=1.0,
         scalar2=0.0,
         op0=MULT,
@@ -330,7 +330,7 @@ def tile_attentionblock_pc_t_kernel(
             )
             store(out_1, b, i, ff_out[b])
 
-        wm_raw = [wstage.tile([P, PACK, 2 * P], BF16, name="wm_raw0"), wstage.tile([P, PACK, 2 * P], BF16, name="wm_raw1")]
+        wm_raw = wstage.tile([P, PACK, FEATS], BF16)
         w1_raw = wstage.tile([P, PACK, FEATS], BF16)
         wm_grouped = wstage.tile([P, FEATS, PACK], BF16, align_bytes=64)
         w1_grouped = wstage.tile([P, FEATS, PACK], BF16, align_bytes=64)
@@ -345,18 +345,12 @@ def tile_attentionblock_pc_t_kernel(
         make_identity(nc, ident_f32[:])
         nc.gpsimd.memset(b1_row[:], 0.0)
 
-        def load_wm(half):
-            cols = slice(half * 2 * P, (half + 1) * 2 * P)
-            for u in range(2):
-                nc.sync.dma_start(
-                    out=wm_raw[half][:, 2 * u : 2 * u + 2, :],
-                    in_=W_merge.rearrange("(u q e) c -> u q e c", u=2, e=2)[u, :, :, cols],
-                )
-
-        load_wm(0)
         load(0, attn_out, 0)
+        nc.sync.dma_start(
+            out=wm_raw[:].rearrange("q (u e) c -> q u (e c)", u=2),
+            in_=W_merge.rearrange("(u q e) c -> q u (e c)", u=2, e=2),
+        )
         load(0, x, 0)
-        load_wm(1)
         nc.sync.dma_start(out=vec_rows[0:2, :], in_=b_merge.rearrange("(u w) -> u w", u=2))
         nc.sync.dma_start(out=vec_rows[2:4, :], in_=gamma2.rearrange("a b (u w) -> (a b u) w", u=2))
         nc.sync.dma_start(out=vec_rows[4:6, :], in_=beta2.rearrange("a b (u w) -> (a b u) w", u=2))
@@ -389,14 +383,14 @@ def tile_attentionblock_pc_t_kernel(
         warm = keep.tile([P, 1], F32)
         nc.scalar.activation(out=warm[:], in_=eps_col[:], func=ACT.Sqrt)
 
-        group_pairs(nc, wm_grouped, wm_raw[0], 0)
+        group_pairs(nc, wm_grouped, wm_raw[:, :, 0 : 2 * P], 0)
         quantise_columns(nc, wm_codes, wm_scales, wm_grouped, slice(0, 2 * P))
         transpose_attn(0, 0)
         transpose_attn(0, 1)
         evict_attn(0, 0)
         evict_attn(0, 1, by_vector=True)
         quantise_attn(0, 0)
-        group_pairs(nc, wm_grouped, wm_raw[1], 1)
+        group_pairs(nc, wm_grouped, wm_raw[:, :, 2 * P : FEATS], 1)
         quantise_columns(nc, wm_codes, wm_scales, wm_grouped, slice(2 * P, FEATS))
         transpose_x(0, 0, 0)
         evict_x(0, 0, 0)

import concourse.mybir as mybir
from concourse.masks import make_identity

F32 = mybir.dt.float32
BF16 = mybir.dt.bfloat16
U32 = mybir.dt.uint32
U8 = mybir.dt.uint8
FP8X4 = mybir.dt.float8_e4m3fn_x4
ADD = mybir.AluOpType.add
MULT = mybir.AluOpType.mult
POW = mybir.AluOpType.pow
ACT = mybir.ActivationFunctionType

P = 128
PACK = 4
BATCH = 4
TOKENS = 1024
FEATS = 512
TILES = TOKENS // P
HALF_TILES = TILES // 2
HALF = HALF_TILES * P
EPS = 1e-5
RUN = 4
WORDS = FEATS // 2

STORE = 2

LEAD = 0
RING = 4

FLOPS = 2 * 2 * BATCH * TOKENS * FEATS * FEATS


def group_pairs(nc, grouped, raw, u):
    by_pair = raw.rearrange("p t (m e) -> p e m t", e=2)
    for e in range(2):
        chunk = 2 * u + e
        nc.vector.tensor_copy(out=grouped[:, chunk * P : (chunk + 1) * P, :], in_=by_pair[:, e, :, :])


def group_runs(nc, grouped, raw):
    nc.gpsimd.tensor_scalar(
        out=grouped[:],
        in0=raw[:].rearrange("p t c -> p c t"),
        scalar1=1.0,
        scalar2=0.0,
        op0=MULT,
        op1=ADD,
    )


def quantise_columns(nc, codes, scales, grouped, cols):
    nc.vector.quantize_mx(
        out=codes[:, cols].bitcast(FP8X4),
        scales=scales[:, cols],
        in_=grouped[:, cols, :].rearrange("p c t -> p (c t)"),
    )


def tile_attentionblock_pc_t_kernel(
    tc, attn_out, x, W_merge, b_merge, gamma2, beta2, W1, b1, out_0, out_1
):
    nc = tc.nc
    with (
        tc.tile_pool(name="keep", bufs=1) as keep,
        tc.tile_pool(name="wstage", bufs=1) as wstage,
        tc.tile_pool(name="inputs", bufs=3) as inputs,
        tc.tile_pool(name="feat", bufs=2) as feat,
        tc.tile_pool(name="x2", bufs=3) as x2_pool,
        tc.tile_pool(name="mx", bufs=2) as mx,
        tc.tile_pool(name="xn", bufs=4) as xn_pool,
        tc.tile_pool(name="outs", bufs=6) as outs,
        tc.tile_pool(name="small", bufs=2) as small,
        tc.psum_pool(name="psum_tr", bufs=4) as psum_tr,
        tc.psum_pool(name="psum_mm", bufs=4) as psum_mm,
        tc.manual_schedule(),
    ):
        attn_sb = {}
        x_sb = {}
        xT = {}
        x2T = {}
        sums = {}
        neg_mean = {}
        ssq = {}
        std = {}
        gain = {}
        shift = {}
        xn = {}
        x2_out = {}
        ff_out = {}
        a_grouped = {}
        a_codes = {}
        a_scales = {}
        n_grouped = {}
        n_codes = {}
        n_scales = {}
        y_ps = {}
        tr_ps = {}
        ff_ps = {}

        def load(b, dram, h):
            if h == 0 and dram is attn_out:
                attn_sb[b] = inputs.tile([P, TILES * FEATS], BF16, name="a_in")
            elif h == 0:
                x_sb[b] = inputs.tile([P, TILES * FEATS], BF16, name="x_in")
            sb = attn_sb[b] if dram is attn_out else x_sb[b]
            width = HALF_TILES * FEATS
            cols = slice(h * width, (h + 1) * width)
            nc.sync.dma_start(
                out=sb[:, cols], in_=dram[b].rearrange("(p i) f -> p (i f)", i=TILES)[:, cols]
            )

        def transpose_attn(b, group):
            a32 = attn_sb[b][:].bitcast(F32)
            at_ps = psum_tr.tile([P, 2, 2 * P], F32, tag="tr")
            for j in range(2):
                i = group * 2 + j
                for u in range(2):
                    nc.tensor.transpose(
                        out=at_ps[:, u, j * P : (j + 1) * P],
                        in_=a32[:, i * WORDS + u * P : i * WORDS + (u + 1) * P],
                        identity=ident_f32[:],
                    )
            tr_ps["A", b, group] = at_ps

        def evict_attn(b, group, by_vector=False):
            h, pair = divmod(group, HALF_TILES // 2)
            if pair == 0:
                a_grouped[b, h] = mx.tile([P, HALF * PACK], BF16, align_bytes=64, name="a_grouped")
            a_words = a_grouped[b, h][:].bitcast(F32).rearrange("p (r u) -> p r u", u=2)
            at_ps = tr_ps["A", b, group]
            (nc.vector.tensor_copy if by_vector else nc.scalar.copy)(
                out=a_words[:, pair * 2 * P : (pair + 1) * 2 * P, :],
                in_=at_ps[:].rearrange("p u r -> p r u"),
            )

        def transpose_x(b, u, h):
            x32 = x_sb[b][:].bitcast(F32)
            xt_ps = psum_tr.tile([P, HALF], F32, tag="tr")
            for j in range(HALF_TILES):
                i = h * HALF_TILES + j
                nc.tensor.transpose(
                    out=xt_ps[:, j * P : (j + 1) * P],
                    in_=x32[:, i * WORDS + u * P : i * WORDS + (u + 1) * P],
                    identity=ident_f32[:],
                )
            tr_ps["X", b, u, h] = xt_ps

        def evict_x(b, u, h, by_vector=False):
            if b not in xT:
                xT[b] = feat.tile([P, 2, TOKENS], F32, name="xT")
            xt_ps = tr_ps["X", b, u, h]
            (nc.vector.tensor_copy if by_vector else nc.scalar.copy)(
                out=xT[b][:, u, h * HALF : (h + 1) * HALF], in_=xt_ps[:]
            )

        def quantise_attn(b, h):
            codes = mx.tile([P, HALF], U32, align_bytes=64, name="a_codes")
            scales = mx.tile([P, HALF], U8, align_bytes=64, name="a_scales")
            nc.vector.quantize_mx(
                out=codes[:].bitcast(FP8X4), scales=scales[:], in_=a_grouped[b, h][:]
            )
            a_codes[b, h] = codes
            a_scales[b, h] = scales

        def first_matmul(b, t, h):
            y_ps[b, t, h] = psum_mm.tile([P, HALF], F32, tag="mm", name="y_ps")
            nc.tensor.matmul_mx(
                out=y_ps[b, t, h][:],
                lhsT=wm_codes[:, t * P : (t + 1) * P].bitcast(FP8X4),
                lhsT_scale=wm_scales[:, t * P : (t + 1) * P],
                rhs=a_codes[b, h][:].bitcast(FP8X4),
                rhs_scale=a_scales[b, h][:],
                start=True,
                stop=True,
            )

        def residual(b, t, h):
            if b not in x2T:
                x2T[b] = x2_pool.tile([P, PACK, TOKENS], F32, name="x2T")
                sums[b] = small.tile([P, PACK, 2], F32, name="sums")
                neg_mean[b] = small.tile([P, PACK], F32, name="neg_mean")
                ssq[b] = small.tile([P, PACK], F32, name="ssq")
            cols = slice(h * HALF, (h + 1) * HALF)
            u, e = divmod(t, 2)
            x_half = xT[b][:, u, cols].bitcast(BF16).rearrange("p (r e) -> p e r", e=2)
            nc.vector.scalar_tensor_tensor(
                out=x2T[b][:, t, cols],
                in0=y_ps[b, t, h][:],
                scalar=bias_m[:, t : t + 1],
                in1=x_half[:, e, :],
                op0=ADD,
                op1=ADD,
                accum_out=sums[b][:, t, h : h + 1],
            )

        def mean(b, t):
            nc.vector.tensor_scalar(
                out=neg_mean[b][:, t : t + 1],
                in0=sums[b][:, t, 0:1],
                scalar1=sums[b][:, t, 1:2],
                scalar2=-1.0 / TOKENS,
                op0=ADD,
                op1=MULT,
            )

        def squares_of(b, t):
            squares = feat.tile([P, TOKENS], BF16, name="squares")
            nc.scalar.activation(
                out=squares[:],
                in_=x2T[b][:, t, :],
                func=ACT.Square,
                bias=neg_mean[b][:, t : t + 1],
                scale=1.0,
                accum_out=ssq[b][:, t : t + 1],
            )

        def std_of(b):
            std[b] = small.tile([P, PACK], F32, name="std")
            nc.scalar.activation(
                out=std[b][:], in_=ssq[b][:], func=ACT.Sqrt, bias=eps_col[:], scale=1.0 / TOKENS
            )

        def affine_step(b, step):
            if step == 0:
                gain[b] = small.tile([P, PACK], F32, name="gain")
                shift[b] = small.tile([P, PACK], F32, name="shift")
                nc.vector.reciprocal(out=gain[b][:], in_=std[b][:])
            elif step == 1:
                nc.vector.tensor_tensor(out=gain[b][:], in0=gain[b][:], in1=gamma, op=MULT)
            elif step == 2:
                nc.vector.tensor_tensor(out=shift[b][:], in0=neg_mean[b][:], in1=gain[b][:], op=MULT)
            else:
                nc.vector.tensor_tensor(out=shift[b][:], in0=shift[b][:], in1=beta, op=ADD)

        def affine_by_gpsimd(b):
            gain[b] = small.tile([P, PACK], F32, name="gain")
            shift[b] = small.tile([P, PACK], F32, name="shift")
            g, s = gain[b][:], shift[b][:]
            nc.gpsimd.tensor_scalar(
                out=g, in0=ssq[b][:], scalar1=1.0 / TOKENS, scalar2=EPS, op0=MULT, op1=ADD
            )
            nc.gpsimd.tensor_tensor(out=g, in0=g, in1=neg_half[:], op=POW)
            nc.gpsimd.tensor_tensor(out=g, in0=g, in1=gamma, op=MULT)
            nc.gpsimd.tensor_tensor(out=s, in0=neg_mean[b][:], in1=g, op=MULT)
            nc.gpsimd.tensor_tensor(out=s, in0=s, in1=beta, op=ADD)

        def norm(b, t, h, engine):
            if (b, h) not in xn:
                xn[b, h] = xn_pool.tile([P, 2, HALF, 2], BF16, align_bytes=64, name="xn")
            cols = slice(h * HALF, (h + 1) * HALF)
            if engine == "scalar":
                nc.scalar.activation(
                    out=xn[b, h][:, t // 2, :, t % 2],
                    in_=x2T[b][:, t, cols],
                    func=ACT.Identity,
                    bias=shift[b][:, t : t + 1],
                    scale=gain[b][:, t : t + 1],
                )
            else:
                (nc.vector if engine == "vector" else nc.gpsimd).tensor_scalar(
                    out=xn[b, h][:, t // 2, :, t % 2],
                    in0=x2T[b][:, t, cols],
                    scalar1=gain[b][:, t : t + 1],
                    scalar2=shift[b][:, t : t + 1],
                    op0=MULT,
                    op1=ADD,
                )

        def transpose_x2(b, i):
            x2_ps = psum_tr.tile([P, FEATS], F32, tag="tr")
            for t in range(PACK):
                nc.tensor.transpose(
                    out=x2_ps[:, t * P : (t + 1) * P],
                    in_=x2T[b][:, t, i * P : (i + 1) * P],
                    identity=ident_f32[:],
                )
            tr_ps["J", b, i] = x2_ps

        def evict_x2(b, i):
            if i % STORE == 0:
                x2_out[b] = outs.tile([P, STORE, FEATS], F32, name="x2_out")
            x2_ps = tr_ps["J", b, i]
            nc.scalar.copy(
                out=x2_out[b][:, i % STORE, :].rearrange("p (u m e) -> p u m e", u=2, e=2),
                in_=x2_ps[:].rearrange("p (u e m) -> p u m e", u=2, e=2),
            )
            store(out_0, b, i, x2_out[b])

        def store(dram, b, i, tile_sb):
            if i % STORE == STORE - 1:
                view = dram[b].rearrange("(p i) f -> p i f", i=TILES)
                nc.sync.dma_start(out=view[:, i + 1 - STORE : i + 1, :], in_=tile_sb[:])

        def group_xn(b, h):
            n_grouped[b, h] = mx.tile([P, HALF, PACK], BF16, align_bytes=64, name="n_grouped")
            words = xn[b, h][:].rearrange("p u c e -> p (u c e)").bitcast(F32)
            nc.vector.tensor_copy(
                out=n_grouped[b, h][:].rearrange("p c t -> p (c t)").bitcast(F32).rearrange("p (c u) -> p c u", u=2),
                in_=words.rearrange("p (u c) -> p c u", u=2),
            )

        def quantise_xn(b, h):
            n_codes[b, h] = mx.tile([P, HALF], U32, align_bytes=64, name="n_codes")
            n_scales[b, h] = mx.tile([P, HALF], U8, align_bytes=64, name="n_scales")
            nc.vector.quantize_mx(
                out=n_codes[b, h][:].bitcast(FP8X4),
                scales=n_scales[b, h][:],
                in_=n_grouped[b, h][:].rearrange("p r t -> p (r t)"),
            )

        def second_matmul(b, i):
            h, j = divmod(i, HALF_TILES)
            ff_ps[b, i] = psum_mm.tile([P, FEATS], F32, tag="mm", name="ff_ps")
            nc.tensor.matmul_mx(
                out=ff_ps[b, i][:],
                lhsT=n_codes[b, h][:, j * P : (j + 1) * P].bitcast(FP8X4),
                lhsT_scale=n_scales[b, h][:, j * P : (j + 1) * P],
                rhs=w1_codes[:].bitcast(FP8X4),
                rhs_scale=w1_scales[:],
                start=True,
                stop=True,
            )

        def second_out(b, i):
            if i % STORE == 0:
                ff_out[b] = outs.tile([P, STORE, FEATS], F32, name="ff_out")
            nc.vector.tensor_tensor(
                out=ff_out[b][:, i % STORE, :], in0=ff_ps[b, i][:], in1=b1_all[:], op=ADD
            )
            store(out_1, b, i, ff_out[b])

        wm_raw = wstage.tile([P, PACK, FEATS], BF16)
        w1_raw = wstage.tile([P, PACK, FEATS], BF16)
        wm_grouped = wstage.tile([P, FEATS, PACK], BF16, align_bytes=64)
        w1_grouped = wstage.tile([P, FEATS, PACK], BF16, align_bytes=64)
        wm_codes = keep.tile([P, FEATS], U32, align_bytes=64)
        wm_scales = keep.tile([P, FEATS], U8, align_bytes=64)
        w1_codes = keep.tile([P, FEATS], U32, align_bytes=64)
        w1_scales = keep.tile([P, FEATS], U8, align_bytes=64)
        vec_rows = keep.tile([P, 2 * P], BF16)
        b1_row = keep.tile([P, FEATS], BF16)
        ident_f32 = keep.tile([P, P], F32)
        nc.gpsimd.memset(vec_rows[:], 0.0)
        make_identity(nc, ident_f32[:])
        nc.gpsimd.memset(b1_row[:], 0.0)

        load(0, attn_out, 0)
        nc.sync.dma_start(
            out=wm_raw[:].rearrange("q (u e) c -> q u (e c)", u=2),
            in_=W_merge.rearrange("(u q e) c -> q u (e c)", u=2, e=2),
        )
        load(0, x, 0)
        nc.sync.dma_start(out=vec_rows[0:2, :], in_=b_merge.rearrange("(u w) -> u w", u=2))
        nc.sync.dma_start(out=vec_rows[2:4, :], in_=gamma2.rearrange("a b (u w) -> (a b u) w", u=2))
        nc.sync.dma_start(out=vec_rows[4:6, :], in_=beta2.rearrange("a b (u w) -> (a b u) w", u=2))
        load(0, attn_out, 1)
        load(0, x, 1)
        load(1, attn_out, 0)
        load(1, attn_out, 1)
        load(1, x, 0)
        load(1, x, 1)
        nc.sync.dma_start(
            out=w1_raw[:].rearrange("q (u e) c -> q u (e c)", u=2),
            in_=W1.rearrange("(u q e) c -> q u (e c)", u=2, e=2),
        )
        nc.sync.dma_start(out=b1_row[0:1, :], in_=b1.rearrange("(o n) -> o n", o=1))

        def load_batch(b):
            load(b, attn_out, 0)
            load(b, attn_out, 1)
            load(b, x, 0)
            load(b, x, 1)

        load_batch(2)

        ones = keep.tile([P, P], BF16)
        nc.gpsimd.memset(ones[:], 1.0)
        eps_col = keep.tile([P, 1], F32)
        nc.gpsimd.memset(eps_col[:], EPS)
        neg_half = keep.tile([P, PACK], F32)
        nc.gpsimd.memset(neg_half[:], -0.5)
        warm = keep.tile([P, 1], F32)
        nc.scalar.activation(out=warm[:], in_=eps_col[:], func=ACT.Sqrt)

        group_pairs(nc, wm_grouped, wm_raw[:, :, 0 : 2 * P], 0)
        quantise_columns(nc, wm_codes, wm_scales, wm_grouped, slice(0, 2 * P))
        transpose_attn(0, 0)
        transpose_attn(0, 1)
        evict_attn(0, 0)
        evict_attn(0, 1, by_vector=True)
        quantise_attn(0, 0)
        group_pairs(nc, wm_grouped, wm_raw[:, :, 2 * P : FEATS], 1)
        quantise_columns(nc, wm_codes, wm_scales, wm_grouped, slice(2 * P, FEATS))
        transpose_x(0, 0, 0)
        evict_x(0, 0, 0)
        vec_t = psum_tr.tile([P, P], F32, tag="tr")
        nc.tensor.transpose(out=vec_t[:], in_=vec_rows[:].bitcast(F32), identity=ident_f32[:])
        vec = keep.tile([P, 12], F32)
        nc.scalar.copy(out=vec[:], in_=vec_t[:].bitcast(BF16)[:, 0:12])
        bias_m = vec[:, 0:4]
        gamma = vec[:, 4:8]
        beta = vec[:, 8:12]
        transpose_x(0, 1, 0)
        evict_x(0, 1, 0)
        first_matmul(0, 0, 0)
        first_matmul(0, 1, 0)
        transpose_attn(0, 2)
        transpose_attn(0, 3)
        b1_all = keep.tile([P, FEATS], F32)

        def prepare_w1(part):
            if part == 0:
                group_runs(nc, w1_grouped, w1_raw)
            else:
                quantise_columns(nc, w1_codes, w1_scales, w1_grouped, slice(0, FEATS))

        def spread_b1():
            b1_ps = psum_tr.tile([P, FEATS], F32, tag="tr")
            nc.tensor.matmul(out=b1_ps[:], lhsT=ones[:], rhs=b1_row[:], start=True, stop=True)
            tr_ps["Z"] = b1_ps

        def evict_b1():
            nc.scalar.copy(out=b1_all[:], in_=tr_ps["Z"][:])


        def squares_step(b, t):
            squares_of(b, t)
            if t == PACK - 1 and b in (0, BATCH - 1):
                std_of(b)

        def adds(b):
            entries = []
            for t in range(PACK):
                entries.append([("D", b, t, 0)] + ([("M", b, t - 1)] if t > 0 else []))
                entries.append([("D", b, t, 1)])
            return entries

        def one(*step):
            return [step]

        def two(*step):
            return [[step], None]

        vec = [one("D", 0, 0, 0), one("D", 0, 1, 0), one("D", 0, 2, 0), one("B", 0, 1), one("D", 0, 3, 0)]
        vec += [one("D", 0, 0, 1), one("D", 0, 1, 1)]
        vec += [[("D", 0, 2, 1), ("M", 0, 0)], [("D", 0, 3, 1), ("M", 0, 1)]]
        vec += [[("B", 1, 0), ("M", 0, 2)], [("B", 1, 1), ("M", 0, 3)]]
        sca = [one("A", 0, 2), one("A", 0, 3), one("X", 0, 0, 1), one("X", 0, 1, 1)]
        sca += [one("A", 1, n) for n in range(4)]
        sca += two("E", 0, 0) + [one("X", 1, 0, 0), one("X", 1, 0, 1)] + two("E", 0, 1)
        sca += [one("X", 1, 1, 0), one("X", 1, 1, 1)] + two("E", 0, 2) + two("E", 0, 3)
        gps = [None] * 8 + [one("L", 3), None, None, one("W", 0)]

        vec += adds(1)
        vec += [[("N", 0, 0), ("M", 1, 3), ("N", 0, 1), ("W", 1), ("N", 0, 2)], [("N", 0, 3)], None]
        for h in range(2):
            vec += [[("F", 0, 0, h, "vector"), ("F", 0, 2, h, "vector")], [("F", 0, 1, h, "vector"), ("F", 0, 3, h, "vector")]]
        vec += two("G", 0, 0) + two("G", 0, 1)
        vec += [one("H", 0, 0), one("B", 2, 0), one("H", 0, 1), one("B", 2, 1)]
        sca += [one("J", 0, i) for i in range(0)] + two("E", 1, 0) + two("E", 1, 1)
        sca += [one("A", 2, n) for n in range(4)] + [one("Z",)] + [one("J", 0, i) for i in range(0, 2)]
        sca += [one("X", 2, 0, 0), one("X", 2, 0, 1)] + two("E", 1, 2) + two("E", 1, 3)
        sca += [one("X", 2, 1, 0), one("X", 2, 1, 1)] + [one("J", 0, i) for i in range(2, TILES)]
        vec += [one("I", 0, n) for n in range(TILES)]
        gps += [None] * (len(vec) - TILES + 5 - len(gps)) + [one("Q", 1)]
        gps += [one("F", 1, t, h, "gpsimd") for h in (1, 0) for t in (0, 2, 1, 3)]

        vec += adds(2)
        vec += [[("G", 1, 1), ("M", 2, 3)], None] + two("G", 1, 0) + [one("H", 1, 1), one("B", 3, 0), one("H", 1, 0), one("B", 3, 1)]
        sca += [one("A", 3, 0), one("A", 3, 1)] + two("E", 2, 0) + [one("A", 3, 2), one("A", 3, 3)] + two("E", 2, 1)
        sca += two("E", 2, 2) + [one("J", 1, i) for i in range(2)] + two("E", 2, 3) + [one("J", 1, i) for i in range(2, 2)]
        sca += [one("X", 3, u, h) for u in range(2) for h in range(2)]
        sca += [one("J", 1, i) for i in range(2, TILES)]
        vec += [one("I", 1, n) for n in (4, 5, 6, 7, 0, 1, 2, 3)]
        gps += [None] * (len(vec) - TILES + 2 - len(gps)) + [one("Q", 2)]
        gps += [one("F", 2, t, h, "gpsimd") for h in (1, 0) for t in (0, 2, 1, 3)]

        vec += adds(3)
        vec += [[("G", 2, 1), ("M", 3, 3)], None] + two("G", 2, 0) + [one("H", 2, 1), one("H", 2, 0)]
        sca += [one("J", 2, i) for i in range(4)]
        for t in range(PACK):
            sca += two("E", 3, t)
        vec += [one("I", 2, 4), one("I", 2, 5), one("I", 2, 6), [("I", 2, 7), ("N", 3, 0)], [("I", 2, 0), ("N", 3, 1)], [("I", 2, 1), ("N", 3, 2)], [("I", 2, 2), ("N", 3, 3)]]
        sca += [one("J", 2, i) for i in range(4, TILES)]
        sca += [one("J", 3, i) for i in range(TILES)]
        vec += [[("F", 3, t, h, "vector"), ("F", 3, t + 2, h, "vector")] for h in (1, 0) for t in (0, 1)]
        vec += two("G", 3, 1) + [one("I", 2, 3), one("H", 3, 1)] + two("G", 3, 0) + [one("H", 3, 0)]
        vec += [one("I", 3, i) for i in (4, 5, 6, 7, 0, 1, 2, 3)]

        drains = [s for entry in vec if entry for s in entry if s[0] in ("D", "I")]

        fills = [s for entry in sca if entry for s in entry if s[0] in ("A", "X", "J", "Z")]
        feeders = {"A": transpose_attn, "X": transpose_x, "J": transpose_x2, "Z": spread_b1}
        fill_state = [2, 0]
        state = [2, 0]

        def matmuls_ahead():
            if state[0] > state[1] + RING - 2:
                return
            while state[0] < len(drains) and state[0] < state[1] + RING:
                s = drains[state[0]]
                if s[0] == "D":
                    if (s[1], s[3]) not in a_codes:
                        return
                    first_matmul(*s[1:])
                else:
                    if (s[1], s[2] // HALF_TILES) not in n_codes:
                        return
                    second_matmul(*s[1:])
                state[0] += 1

        def transposes_ahead():
            if fill_state[0] > fill_state[1] + RING - 2:
                return
            while fill_state[0] < len(fills) and fill_state[0] < fill_state[1] + RING:
                s = fills[fill_state[0]]
                if s[0] == "J" and (s[1], PACK - 1, 1) not in added:
                    return
                feeders[s[0]](*[a for a in s[1:] if a is not True])
                fill_state[0] += 1

        added = set()
        does = {
            "A": evict_attn,
            "X": evict_x,
            "Z": evict_b1,
            "B": quantise_attn,
            "D": residual,
            "M": mean,
            "E": squares_step,
            "N": affine_step,
            "Q": affine_by_gpsimd,
            "F": norm,
            "G": group_xn,
            "H": quantise_xn,
            "I": second_out,
            "J": evict_x2,
            "L": load_batch,
            "W": prepare_w1,
        }
        def run(entry):
            for s in entry or []:
                does[s[0]](*s[1:])
                done.add(s)
                if s[0] == "D":
                    added.add(s[1:])
                if s[0] in ("D", "I"):
                    state[1] += 1
                if s[0] in feeders:
                    fill_state[1] += 1

        def needs(s):
            if s[0] == "D":
                return [("X", s[1], s[2] // 2, s[3])]
            if s[0] == "B":
                return [("A", s[1], 2 * s[2]), ("A", s[1], 2 * s[2] + 1)]
            if s[0] in ("N", "Q"):
                return [("E", s[1], PACK - 1)]
            return []

        def startable(entry):
            for s in entry or []:
                if s[0] == "E" and ("M",) + s[1:] not in done:
                    return False
                if s[0] == "J" and ("D", s[1], PACK - 1, 1) not in done:
                    return False
                if s[0] == "F" and ("N", s[1], 3) not in done:
                    return False
            return True

        done = set()
        sca_steps = set([s for entry in sca if entry for s in entry])
        at = 0
        for n in range(max(len(vec), len(gps))):
            matmuls_ahead()
            transposes_ahead()
            entry = vec[n] if n < len(vec) else None
            for s in entry or []:
                while not all(need in done for need in needs(s) if need in sca_steps):
                    transposes_ahead()
                    run(sca[at])
                    at += 1
            run(entry)
            matmuls_ahead()
            while at < len(sca) and at < n + 1 + LEAD and startable(sca[at]):
                transposes_ahead()
                run(sca[at])
                at += 1
            entry = gps[n] if n < len(gps) else None
            for s in entry or []:
                while not all(need in done for need in needs(s) if need in sca_steps):
                    transposes_ahead()
                    run(sca[at])
                    at += 1
            run(entry)
        while at < len(sca):
            transposes_ahead()
            run(sca[at])
            at += 1
